import numpy as np
import ml_dtypes


def mxq(x, axis, fmt="e4m3"):
    dtype, down = {"e4m3": (ml_dtypes.float8_e4m3fn, 7), "e5m2": (ml_dtypes.float8_e5m2, 14)}[fmt]
    v = np.moveaxis(np.asarray(x, np.float32).astype(ml_dtypes.bfloat16).astype(np.float64), axis, -1)
    blocks = v.reshape(v.shape[:-1] + (-1, 32))
    amax = np.abs(blocks).max(-1, keepdims=True)
    byte = np.maximum(np.where(amax > 0, np.frexp(amax)[1] - 1 + 127, 0) - down, 1)
    scale = np.exp2(byte - 127.0)
    codes = (blocks / scale).astype(np.float32).astype(dtype).astype(np.float64)
    return np.moveaxis((codes * scale).reshape(v.shape), -1, axis)


WIDE = False


def mx_kscale(k):
    if not WIDE:
        return np.ones(k)
    levels = np.array([10, -10, 5, -5, 0])
    if k % 512:
        return np.exp2(np.random.permutation(np.resize(levels, k // 32))).repeat(32)
    a = np.empty((k // 512, 16))
    for p in range(k // 512):
        a[p, :8] = np.random.permutation(np.resize(levels, 8))
        for g in range(8):
            far = levels[np.abs(levels - a[p, g]) >= 10]
            a[p, g + 8] = far[np.random.randint(len(far))]
    return np.exp2(a.ravel()).repeat(32)


BF16 = ml_dtypes.bfloat16


def bf(x):
    return np.asarray(x, np.float32).astype(BF16)


def f64(x):
    return np.asarray(x).astype(np.float64)


B, N, D, H, L, C = 4, 512, 512, 8, 3, 2
HD = D // H


def setup_inputs():
    s, t = mx_kscale(D), mx_kscale(D)
    tk = t.reshape(H, HD)[:, :L]
    return {
        "fields": bf((np.random.standard_normal((B, N, D)) + np.random.standard_normal((B, 1, D))) * t),
        "h2": bf(np.maximum(np.random.standard_normal((B, N, D)), 0.0) * 1.4 * s),
        "corr_kernels": bf(np.random.standard_normal((H, L, L)) * 2.5 / tk[:, None, :]),
        "w3": bf(np.random.standard_normal((D, D)) * 1.5 / np.sqrt(D) * t[:, None] / s[None, :]),
        "b3": bf(np.random.standard_normal(D) * 0.3 * t),
        "out_w": bf(np.random.standard_normal((D, D)) / np.sqrt(D) / t[None, :]),
        "out_b": bf(np.random.standard_normal(D) * 0.3),
        "inter_w": bf(1.0 + 0.5 * np.random.standard_normal(C)),
    }


def reference(fields, h2, corr_kernels, w3, b3, out_w, out_b, inter_w):
    f = f64(fields).reshape(B, N, H, HD)
    ck = f64(corr_kernels)
    corr = np.zeros((B, N, H, HD))
    for lag in range(1, L + 1):
        base = f[:, :-lag]
        shifted = f[:, lag:]
        w = np.pad(ck[:, lag - 1, :], ((0, 0), (0, HD - L)))
        mean_shift = shifted.mean(axis=1, keepdims=True)
        cw = base * w[None, None] * mean_shift
        corr = corr + np.pad(cw, ((0, 0), (0, lag), (0, 0), (0, 0)))
    corr = corr / L
    nl = ((mxq(f64(h2), 2, "e4m3") @ mxq(f64(w3), 1, "e4m3").T) + f64(b3)).reshape(B, N, H, HD)
    r = f64(inter_w)
    e = np.exp(r - r.max())
    iw = e / e.sum()
    enhanced = (f + iw[0] * corr + iw[1] * nl).reshape(B, N, D)
    return (mxq(enhanced, 2, "e4m3") @ mxq(f64(out_w), 1, "e4m3").T) + f64(out_b)

@@ -1,0 +1,382 @@
+import concourse.mybir as mybir
+from concourse.masks import make_identity
+
+F32 = mybir.dt.float32
+BF16 = mybir.dt.bfloat16
+U32 = mybir.dt.uint32
+U8 = mybir.dt.uint8
+FP8X4 = mybir.dt.float8_e4m3fn_x4
+ALU = mybir.AluOpType
+ACT = mybir.ActivationFunctionType
+AXIS = mybir.AxisListType
+
+B, N, D, H, L = 4, 512, 512, 8, 3
+HD = D // H
+P = 128
+PACK = 4
+TILES = 4
+ALL = B * TILES
+SCALAR_TILES = ()
+
+FLOPS = 2 * 2 * B * N * D * D
+
+
+def alternate_words(rows, u):
+    return rows.bitcast(F32).rearrange("r (p u) -> r u p", u=2)[:, u, :]
+
+
+def flip_two_row_tiles(nc, bank, rows2, words, ident_f32):
+    for g in range(2):
+        for u in range(2):
+            nc.tensor.transpose(bank[:, g, u, :], words(rows2[:, g, :], u), ident_f32[:])
+
+
+def copy_two_row_tiles(copy_out, grouped, pair, bank):
+    copy_out(
+        out=grouped[:].bitcast(F32)[:, 2 * pair : 2 * pair + 2, :, :], in_=bank[:].rearrange("p g u r -> p g r u")
+    )
+
+
+def quantise_rows(nc, grouped, codes, scales):
+    nc.vector.quantize_mx(
+        out=codes.bitcast(FP8X4), scales=scales, in_=grouped[:].rearrange("p g r t -> p (g r t)")
+    )
+
+
+def batch_due(g, lead):
+    b, rest = divmod(g + lead, TILES)
+    return b if rest == 0 and b < B else None
+
+
+def tile_fieldinteractionoperators_pa_kernel(
+    tc, fields, h2, corr_kernels, w3, b3, out_w, out_b, inter_w, out
+):
+    nc = tc.nc
+    with (
+        tc.tile_pool(name="keep", bufs=1) as keep,
+        tc.tile_pool(name="stage", bufs=2) as stage,
+        tc.tile_pool(name="results", bufs=4) as results,
+        tc.psum_pool(name="psum_flip", bufs=2) as psum_flip,
+        tc.psum_pool(name="psum_field", bufs=2) as psum_field,
+        tc.psum_pool(name="psum_first", bufs=2) as psum_first,
+        tc.psum_pool(name="psum_second", bufs=2) as psum_second,
+        tc.manual_schedule(),
+    ):
+        ident_f32 = keep.tile([P, P], F32)
+        make_identity(nc, ident_f32[:])
+        ones = keep.tile([P, P], BF16)
+        nc.vector.memset(ones[:], 1.0)
+        out_b_row = keep.tile([P, D], BF16)
+        nc.vector.memset(out_b_row[:], 0.0)
+        zero = keep.tile([P, 1], F32)
+        nc.vector.memset(zero[:], 0.0)
+        token_weights = keep.tile([P, TILES, 2 * L], BF16)
+        nc.vector.memset(token_weights[:], 0.0)
+        nc.vector.memset(token_weights[:, :, 0:L], 1.0)
+        for s in range(L):
+            nc.vector.memset(token_weights[0:1, 0 : L - s, s : s + 1], 0.0)
+        for a in range(L):
+            nc.vector.tensor_copy(out=token_weights[:, a + 1, L + a : L + a + 1], in_=ident_f32[:, P - 1 : P])
+
+        kernels_all = keep.tile([P, H, L * L], BF16)
+        mix = keep.tile([P, 2], BF16)
+        b3_pt = keep.tile([P, PACK], BF16)
+        f_nat = keep.tile([P, B, TILES, D], BF16)
+        h_nat = keep.tile([P, B, TILES, D], BF16)
+        w3_nat = keep.tile([P, TILES, D], BF16)
+        ow_nat = keep.tile([P, TILES, D], BF16)
+
+        def load_tokens(tile, tensor, b):
+            nc.sync.dma_start(out=tile[:, b], in_=tensor[b].rearrange("(q i) c -> q i c", i=TILES))
+
+        nc.scalar.dma_start(
+            out=kernels_all[:].rearrange("p h x -> p (h x)"),
+            in_=corr_kernels.rearrange("h l j -> (h l j)").partition_broadcast(P),
+        )
+        nc.scalar.dma_start(out=mix[:], in_=inter_w.partition_broadcast(P))
+        nc.scalar.dma_start(out=b3_pt[:], in_=b3.rearrange("(p t) -> p t", t=PACK))
+        nc.scalar.dma_start(out=out_b_row[0:1, :], in_=out_b.unsqueeze(0))
+        load_tokens(f_nat, fields, 0)
+        nc.sync.dma_start(out=w3_nat[:], in_=w3.rearrange("(p t) k -> p t k", t=TILES))
+        load_tokens(h_nat, h2, 0)
+        nc.sync.dma_start(out=ow_nat[:], in_=out_w.rearrange("(g r) c -> r g c", r=P))
+        for b in range(1, B):
+            load_tokens(f_nat, fields, b)
+            load_tokens(h_nat, h2, b)
+
+        warm = keep.tile([P, 1], F32)
+        nc.scalar.activation(out=warm[:], in_=zero[:], func=ACT.Exp)
+
+        neg_top = keep.tile([P, 1], F32)
+        nc.vector.tensor_max(out=neg_top[:], in0=mix[:, 0:1], in1=mix[:, 1:2])
+        nc.vector.tensor_scalar_mul(out=neg_top[:], in0=neg_top[:], scalar1=-1.0)
+        expd = keep.tile([P, 2], F32)
+        total = keep.tile([P, 1], F32)
+        nc.scalar.activation(out=expd[:], in_=mix[:], func=ACT.Exp, bias=neg_top[:, 0:1], scale=1.0, accum_out=total[:])
+
+        own_head = ident_f32[:].rearrange("p (h r) -> p h r", r=P // H)[:, :, 0]
+        by_head = keep.tile([P, L * L, H], F32)
+        nc.vector.tensor_tensor(
+            out=by_head[:],
+            in0=kernels_all[:].rearrange("p h x -> p x h"),
+            in1=own_head.unsqueeze(1).to_broadcast([P, L * L, H]),
+            op=ALU.mult,
+        )
+        kernels_own = keep.tile([P, L, L], F32)
+        nc.vector.tensor_reduce(out=kernels_own[:].rearrange("p l j -> p (l j)"), in_=by_head[:], axis=AXIS.X, op=ALU.add)
+        kappa = keep.tile([P, L, L + 1, L], F32)
+        nc.vector.memset(kappa[:], 0.0)
+        for s in range(L):
+            lag = L - s
+            nc.vector.tensor_scalar_mul(
+                out=kappa[:, :, L, s], in0=kernels_own[:, lag - 1, :], scalar1=1.0 / (L * (N - lag))
+            )
+        for a in range(L):
+            nc.vector.tensor_copy(out=kappa[:, :, a, 0 : a + 1], in_=kappa[:, :, L, 0 : a + 1])
+        terms = keep.tile([P, L, L + 1, L + 1], F32)
+        nc.vector.memset(terms[:], 0.0)
+        nc.vector.memset(terms[:, :, L, L : L + 1], 1.0)
+
+        nc.vector.reciprocal(out=total[:], in_=total[:])
+        iw = keep.tile([P, 2], F32)
+        nc.vector.tensor_scalar_mul(out=iw[:], in0=expd[:], scalar1=total[:, 0:1])
+        bias_pt = keep.tile([P, PACK], F32)
+        nc.vector.tensor_scalar_mul(out=bias_pt[:], in0=b3_pt[:], scalar1=iw[:, 1:2])
+        nc.vector.tensor_scalar_mul(out=kappa[:], in0=kappa[:], scalar1=iw[:, 0:1])
+
+        gains = keep.tile([P, B, L, L + 1], F32)
+        sums = {}
+        lacking = {}
+
+        def sum_fields(b):
+            bank = psum_flip.tile([P, L, 2 * L], F32, tag="flipped")
+            for t in range(L):
+                for i in range(TILES):
+                    nc.tensor.matmul(
+                        out=bank[:, t, :],
+                        lhsT=f_nat[:, b, i, :].rearrange("q (p t) -> q t p", t=PACK)[:, t, :],
+                        rhs=token_weights[:, i, :],
+                        start=(i == 0),
+                        stop=(i == TILES - 1),
+                    )
+            sums[b] = bank
+
+        def weigh_sums(b):
+            nc.vector.tensor_tensor(
+                out=terms[:, :, :, 0:L],
+                in0=sums[b][:, :, 0:L].unsqueeze(2).to_broadcast([P, L, L + 1, L]),
+                in1=kappa[:],
+                op=ALU.mult,
+            )
+
+        def add_terms(b):
+            nc.vector.tensor_reduce(out=gains[:, b], in_=terms[:], axis=AXIS.X, op=ALU.add)
+
+        def find_lacking(b):
+            lack = stage.tile([P, L, L], F32, tag="lacking")
+            nc.vector.tensor_tensor(out=lack[:], in0=sums[b][:, :, L : 2 * L], in1=gains[:, b, :, 0:L], op=ALU.mult)
+            lacking[b] = lack
+
+        field_banks = {}
+        scaled = {}
+        hidden_banks = {}
+        h_grouped = {}
+        h_codes = {}
+        h_scales = {}
+
+        def flip_fields(b):
+            for u in range(2):
+                flipped_f = psum_field.tile([P, TILES, P], F32, tag="fields")
+                for i in range(TILES):
+                    nc.tensor.transpose(flipped_f[:, i, :], alternate_words(f_nat[:, b, i, :], u), ident_f32[:])
+                field_banks[(b, u)] = flipped_f
+            scaled_b = stage.tile([P, PACK, N], F32, tag="scaled")
+            scaled[b] = scaled_b
+
+        def scale_fields(b, t):
+            u, e = divmod(t, 2)
+            halves = field_banks[(b, u)][:].bitcast(BF16).rearrange("p i (q e) -> p (i q) e", e=2)
+            nc.scalar.activation(
+                out=scaled[b][:, t, :],
+                in_=halves[:, :, e],
+                func=ACT.Identity,
+                scale=gains[:, b, t, L : L + 1] if t < L else 1.0,
+                bias=bias_pt[:, t : t + 1],
+            )
+
+        def mend_last_tokens(b):
+            last_columns = scaled[b][:, 0:L, :].rearrange("p t (i q) -> p t i q", q=P)[:, :, 1:TILES, P - 1]
+            nc.vector.tensor_tensor(out=last_columns, in0=last_columns, in1=lacking[b][:], op=ALU.subtract)
+
+        def flip_hidden(b):
+            for pair in range(2):
+                bank = psum_flip.tile([P, 2, 2, P], F32, tag="flipped")
+                flip_two_row_tiles(nc, bank, h_nat[:, b, 2 * pair : 2 * pair + 2, :], alternate_words, ident_f32)
+                hidden_banks[(b, pair)] = bank
+            grouped = stage.tile([P, TILES, P, PACK], BF16, align_bytes=64, tag="grouped")
+            h_grouped[b] = grouped
+
+        def copy_hidden(copy_out, b, pair):
+            copy_two_row_tiles(copy_out, h_grouped[b], pair, hidden_banks[(b, pair)])
+
+        def quantise_hidden(b):
+            codes = stage.tile([P, N], U32, align_bytes=64, tag="h_codes")
+            planes = stage.tile([P, N], U8, align_bytes=64, tag="h_scales")
+            quantise_rows(nc, h_grouped[b], codes[:], planes[:])
+            h_codes[b], h_scales[b] = codes, planes
+
+        def flip_weight(pool, tag, rows4, words):
+            banks = []
+            for pair in range(2):
+                bank = pool.tile([P, 2, 2, P], F32, tag=tag, name="weight_bank")
+                flip_two_row_tiles(nc, bank, rows4[:, 2 * pair : 2 * pair + 2, :], words, ident_f32)
+                banks.append(bank)
+            return banks
+
+        def copy_weight(banks):
+            grouped = stage.tile([P, TILES, P, PACK], BF16, align_bytes=64, tag="grouped")
+            for pair in range(2):
+                copy_two_row_tiles(nc.scalar.copy, grouped, pair, banks[pair])
+            return grouped
+
+        nl = {}
+        enhanced = {}
+        e_codes = {}
+        e_scales = {}
+        acc = {}
+
+        def first_product(g):
+            b, i = divmod(g, TILES)
+            tokens = slice(i * P, (i + 1) * P)
+            bank = psum_first.tile([P, PACK, P], F32, tag="nl")
+            for t in range(PACK):
+                channels = slice(t * P, (t + 1) * P)
+                nc.tensor.matmul_mx(
+                    out=bank[:, t, :],
+                    lhsT=w3_codes[:, channels].bitcast(FP8X4),
+                    lhsT_scale=w3_scales[:, channels],
+                    rhs=h_codes[b][:, tokens].bitcast(FP8X4),
+                    rhs_scale=h_scales[b][:, tokens],
+                    start=True,
+                    stop=True,
+                )
+            nl[g] = bank
+
+        def fuse(g):
+            b, i = divmod(g, TILES)
+            fused = results.tile([P, P, PACK], BF16, align_bytes=64, tag="fused")
+            nc.vector.scalar_tensor_tensor(
+                out=fused[:],
+                in0=nl[g][:].rearrange("p t q -> p q t"),
+                scalar=iw[:, 1:2],
+                in1=scaled[b][:, :, i * P : (i + 1) * P].rearrange("p t q -> p q t"),
+                op0=ALU.mult,
+                op1=ALU.add,
+            )
+            enhanced[g] = fused
+
+        def quantise_enhanced(g):
+            codes = results.tile([P, P], U32, align_bytes=64, tag="e_codes")
+            planes = results.tile([P, P], U8, align_bytes=64, tag="e_scales")
+            nc.vector.quantize_mx(
+                out=codes[:].bitcast(FP8X4), scales=planes[:], in_=enhanced[g][:].rearrange("p q t -> p (q t)")
+            )
+            e_codes[g], e_scales[g] = codes, planes
+
+        def second_product(g):
+            bank = psum_second.tile([P, D], F32, tag="acc")
+            nc.tensor.matmul_mx(
+                out=bank[:],
+                lhsT=e_codes[g][:].bitcast(FP8X4),
+                lhsT_scale=e_scales[g][:],
+                rhs=ow_codes[:].bitcast(FP8X4),
+                rhs_scale=ow_scales[:],
+                start=True,
+                stop=True,
+            )
+            acc[g] = bank
+
+        def finish(g):
+            b, i = divmod(g, TILES)
+            result = results.tile([P, D], F32, tag="result")
+            if i in SCALAR_TILES:
+                nc.scalar.copy(out=result[:], in_=acc[g][:])
+                nc.gpsimd.tensor_tensor(out=result[:], in0=result[:], in1=out_b_all[:], op=ALU.add)
+            else:
+                nc.vector.tensor_tensor(out=result[:], in0=acc[g][:], in1=out_b_all[:], op=ALU.add)
+            nc.sync.dma_start(out=out[b].rearrange("(q i) o -> q i o", i=TILES)[:, i, :], in_=result[:])
+
+        sum_fields(0)
+        weigh_sums(0)
+        add_terms(0)
+        find_lacking(0)
+        w3_banks = flip_weight(psum_first, "nl", w3_nat[:], alternate_words)
+        w3_grouped = copy_weight(w3_banks)
+        flip_fields(0)
+        for t in range(PACK):
+            scale_fields(0, t)
+        flip_hidden(0)
+        w3_codes = keep.tile([P, D], U32, align_bytes=64)
+        w3_scales = keep.tile([P, D], U8, align_bytes=64)
+        quantise_rows(nc, w3_grouped, w3_codes[:], w3_scales[:])
+        copy_hidden(nc.vector.tensor_copy, 0, 0)
+        copy_hidden(nc.vector.tensor_copy, 0, 1)
+        ow_banks = flip_weight(psum_second, "acc", ow_nat[:], alternate_words)
+        ow_grouped = copy_weight(ow_banks)
+        sum_fields(1)
+        quantise_hidden(0)
+        weigh_sums(1)
+        first_product(0)
+        first_product(1)
+        add_terms(1)
+        spread_out_b = psum_second.tile([P, D], F32, tag="acc")
+        nc.tensor.matmul(out=spread_out_b[:], lhsT=ones[:], rhs=out_b_row[:], start=True, stop=True)
+        out_b_all = keep.tile([P, D], F32)
+        nc.scalar.copy(out=out_b_all[:], in_=spread_out_b[:])
+        find_lacking(1)
+        flip_hidden(1)
+        fuse(0)
+        first_product(2)
+        flip_fields(1)
+        ow_codes = keep.tile([P, D], U32, align_bytes=64)
+        ow_scales = keep.tile([P, D], U8, align_bytes=64)
+        quantise_rows(nc, ow_grouped, ow_codes[:], ow_scales[:])
+        mend_last_tokens(0)
+        copy_hidden(nc.scalar.copy, 1, 0)
+        copy_hidden(nc.scalar.copy, 1, 1)
+
+        for g in range(1, ALL + 2):
+            if batch_due(g, 7) is not None:
+                sum_fields(batch_due(g, 7))
+            if g < ALL:
+                fuse(g)
+            if g < ALL and g % TILES == 0:
+                mend_last_tokens(g // TILES)
+            if batch_due(g, 6) is not None:
+                weigh_sums(batch_due(g, 6))
+            if batch_due(g, 5) is not None:
+                find_lacking(batch_due(g, 5))
+                flip_hidden(batch_due(g, 5))
+            if batch_due(g, 4) is not None:
+                flip_fields(batch_due(g, 4))
+            if g - 1 < ALL:
+                quantise_enhanced(g - 1)
+                second_product(g - 1)
+            if batch_due(g, 6) is not None:
+                add_terms(batch_due(g, 6))
+            if batch_due(g, 3) is not None:
+                quantise_hidden(batch_due(g, 3))
+            if g + 2 < ALL:
+                first_product(g + 2)
+            if g - 2 >= 0:
+                finish(g - 2)
+            if batch_due(g, 4) is not None:
+                copy_hidden(nc.scalar.copy, batch_due(g, 4), 0)
+                copy_hidden(nc.scalar.copy, batch_due(g, 4), 1)
+            if batch_due(g, 3) is not None:
+                scale_fields(batch_due(g, 3), 0)
+                scale_fields(batch_due(g, 3), 1)
+            if batch_due(g, 2) is not None:
+                scale_fields(batch_due(g, 2), 2)
+            if batch_due(g, 1) is not None:
+                scale_fields(batch_due(g, 1), 3)

@@ -11,12 +11,17 @@ ACT = mybir.ActivationFunctionType
 AXIS = mybir.AxisListType
 
 B, N, D, H, L = 4, 512, 512, 8, 3
-HD = D // H
 P = 128
 PACK = 4
 TILES = 4
-ALL = B * TILES
-SCALAR_TILES = ()
+PAIR = 2 * P
+PAIRS = B * TILES // 2
+
+ROW_KERNELS = 0
+ROW_MIX = 80
+ROW_B3 = 96
+ROW_OUT_B = ROW_B3 + D
+ROW_END = ROW_OUT_B + D
 
 FLOPS = 2 * 2 * B * N * D * D
 
@@ -25,27 +30,18 @@ def alternate_words(rows, u):
     return rows.bitcast(F32).rearrange("r (p u) -> r u p", u=2)[:, u, :]
 
 
-def flip_two_row_tiles(nc, bank, rows2, words, ident_f32):
+def flip_pair(nc, bank, rows2, ident_f32):
     for g in range(2):
         for u in range(2):
-            nc.tensor.transpose(bank[:, g, u, :], words(rows2[:, g, :], u), ident_f32[:])
+            nc.tensor.transpose(bank[:, g, u, :], alternate_words(rows2[:, g, :], u), ident_f32[:])
 
 
-def copy_two_row_tiles(copy_out, grouped, pair, bank):
-    copy_out(
-        out=grouped[:].bitcast(F32)[:, 2 * pair : 2 * pair + 2, :, :], in_=bank[:].rearrange("p g u r -> p g r u")
-    )
+def copy_pair(copy_out, grouped, bank):
+    copy_out(out=grouped[:].bitcast(F32), in_=bank[:].rearrange("p g u r -> p g r u"))
 
 
-def quantise_rows(nc, grouped, codes, scales):
-    nc.vector.quantize_mx(
-        out=codes.bitcast(FP8X4), scales=scales, in_=grouped[:].rearrange("p g r t -> p (g r t)")
-    )
-
-
-def batch_due(g, lead):
-    b, rest = divmod(g + lead, TILES)
-    return b if rest == 0 and b < B else None
+def quantise_pair(nc, grouped, codes, scales):
+    nc.vector.quantize_mx(out=codes.bitcast(FP8X4), scales=scales, in_=grouped[:].rearrange("p g r t -> p (g r t)"))
 
 
 def tile_fieldinteractionoperators_pa_kernel(
@@ -54,102 +50,102 @@ def tile_fieldinteractionoperators_pa_kernel(
     nc = tc.nc
     with (
         tc.tile_pool(name="keep", bufs=1) as keep,
-        tc.tile_pool(name="stage", bufs=2) as stage,
+        tc.tile_pool(name="stage", bufs=3) as stage,
         tc.tile_pool(name="results", bufs=4) as results,
-        tc.psum_pool(name="psum_flip", bufs=2) as psum_flip,
-        tc.psum_pool(name="psum_field", bufs=2) as psum_field,
-        tc.psum_pool(name="psum_first", bufs=2) as psum_first,
+        tc.psum_pool(name="psum_flip", bufs=3) as psum_flip,
+        tc.psum_pool(name="psum_first", bufs=3) as psum_first,
         tc.psum_pool(name="psum_second", bufs=2) as psum_second,
         tc.manual_schedule(),
     ):
-        ident_f32 = keep.tile([P, P], F32)
-        make_identity(nc, ident_f32[:])
-        ones = keep.tile([P, P], BF16)
-        nc.vector.memset(ones[:], 1.0)
-        out_b_row = keep.tile([P, D], BF16)
-        nc.vector.memset(out_b_row[:], 0.0)
-        zero = keep.tile([P, 1], F32)
-        nc.vector.memset(zero[:], 0.0)
-        token_weights = keep.tile([P, TILES, 2 * L], BF16)
-        nc.vector.memset(token_weights[:], 0.0)
-        nc.vector.memset(token_weights[:, :, 0:L], 1.0)
-        for s in range(L):
-            nc.vector.memset(token_weights[0:1, 0 : L - s, s : s + 1], 0.0)
-        for a in range(L):
-            nc.vector.tensor_copy(out=token_weights[:, a + 1, L + a : L + a + 1], in_=ident_f32[:, P - 1 : P])
+        rows = keep.tile([P, ROW_END], BF16)
+        for first, last in ((0, ROW_B3), (ROW_B3, ROW_END)):
+            nc.vector.memset(rows[:, first:last].bitcast(F32), 0.0)
+        nc.scalar.dma_start(
+            out=rows[0:1, ROW_KERNELS : ROW_KERNELS + H * L * L],
+            in_=corr_kernels.rearrange("h l j -> (h l j)").unsqueeze(0),
+        )
+        nc.scalar.dma_start(out=rows[0:1, ROW_MIX : ROW_MIX + 2], in_=inter_w.unsqueeze(0))
+        nc.scalar.dma_start(out=rows[0:1, ROW_B3 : ROW_B3 + D], in_=b3.unsqueeze(0))
+        nc.scalar.dma_start(out=rows[0:1, ROW_OUT_B : ROW_OUT_B + D], in_=out_b.unsqueeze(0))
 
-        kernels_all = keep.tile([P, H, L * L], BF16)
-        mix = keep.tile([P, 2], BF16)
-        b3_pt = keep.tile([P, PACK], BF16)
         f_nat = keep.tile([P, B, TILES, D], BF16)
         h_nat = keep.tile([P, B, TILES, D], BF16)
         w3_nat = keep.tile([P, TILES, D], BF16)
         ow_nat = keep.tile([P, TILES, D], BF16)
 
-        def load_tokens(tile, tensor, b):
-            nc.sync.dma_start(out=tile[:, b], in_=tensor[b].rearrange("(q i) c -> q i c", i=TILES))
+        def load_tokens(tile, tensor, b, first, last):
+            nc.sync.dma_start(
+                out=tile[:, b, first:last], in_=tensor[b].rearrange("(q i) c -> q i c", i=TILES)[:, first:last]
+            )
 
-        nc.scalar.dma_start(
-            out=kernels_all[:].rearrange("p h x -> p (h x)"),
-            in_=corr_kernels.rearrange("h l j -> (h l j)").partition_broadcast(P),
-        )
-        nc.scalar.dma_start(out=mix[:], in_=inter_w.partition_broadcast(P))
-        nc.scalar.dma_start(out=b3_pt[:], in_=b3.rearrange("(p t) -> p t", t=PACK))
-        nc.scalar.dma_start(out=out_b_row[0:1, :], in_=out_b.unsqueeze(0))
-        load_tokens(f_nat, fields, 0)
-        nc.sync.dma_start(out=w3_nat[:], in_=w3.rearrange("(p t) k -> p t k", t=TILES))
-        load_tokens(h_nat, h2, 0)
+        w3_rows = w3.rearrange("(p t) k -> p t k", t=TILES)
+        for half in range(2):
+            nc.sync.dma_start(out=w3_nat[:, 2 * half : 2 * half + 2], in_=w3_rows[:, 2 * half : 2 * half + 2])
+        load_tokens(f_nat, fields, 0, 0, TILES)
+        load_tokens(h_nat, h2, 0, 0, 2)
+        load_tokens(h_nat, h2, 0, 2, TILES)
         nc.sync.dma_start(out=ow_nat[:], in_=out_w.rearrange("(g r) c -> r g c", r=P))
         for b in range(1, B):
-            load_tokens(f_nat, fields, b)
-            load_tokens(h_nat, h2, b)
+            load_tokens(f_nat, fields, b, 0, TILES)
+            load_tokens(h_nat, h2, b, 0, TILES)
 
+        ident_f32 = keep.tile([P, P], F32)
+        make_identity(nc, ident_f32[:])
+        ones = keep.tile([P, P], BF16)
+        nc.vector.memset(ones[:], 1.0)
+        zero = keep.tile([P, 1], F32)
+        nc.vector.memset(zero[:], 0.0)
         warm = keep.tile([P, 1], F32)
         nc.scalar.activation(out=warm[:], in_=zero[:], func=ACT.Exp)
-
-        neg_top = keep.tile([P, 1], F32)
-        nc.vector.tensor_max(out=neg_top[:], in0=mix[:, 0:1], in1=mix[:, 1:2])
-        nc.vector.tensor_scalar_mul(out=neg_top[:], in0=neg_top[:], scalar1=-1.0)
-        expd = keep.tile([P, 2], F32)
-        total = keep.tile([P, 1], F32)
-        nc.scalar.activation(out=expd[:], in_=mix[:], func=ACT.Exp, bias=neg_top[:, 0:1], scale=1.0, accum_out=total[:])
-
-        own_head = ident_f32[:].rearrange("p (h r) -> p h r", r=P // H)[:, :, 0]
-        by_head = keep.tile([P, L * L, H], F32)
-        nc.vector.tensor_tensor(
-            out=by_head[:],
-            in0=kernels_all[:].rearrange("p h x -> p x h"),
-            in1=own_head.unsqueeze(1).to_broadcast([P, L * L, H]),
-            op=ALU.mult,
-        )
-        kernels_own = keep.tile([P, L, L], F32)
-        nc.vector.tensor_reduce(out=kernels_own[:].rearrange("p l j -> p (l j)"), in_=by_head[:], axis=AXIS.X, op=ALU.add)
-        kappa = keep.tile([P, L, L + 1, L], F32)
-        nc.vector.memset(kappa[:], 0.0)
+        token_weights = keep.tile([P, TILES, 2 * L], BF16)
+        nc.vector.memset(token_weights[:], 0.0)
+        nc.vector.memset(token_weights[:, :, 0:L], 1.0)
         for s in range(L):
-            lag = L - s
-            nc.vector.tensor_scalar_mul(
-                out=kappa[:, :, L, s], in0=kernels_own[:, lag - 1, :], scalar1=1.0 / (L * (N - lag))
-            )
+            nc.vector.memset(token_weights[0:1, 0 : s + 1, s : s + 1], 0.0)
         for a in range(L):
-            nc.vector.tensor_copy(out=kappa[:, :, a, 0 : a + 1], in_=kappa[:, :, L, 0 : a + 1])
+            nc.vector.tensor_copy(out=token_weights[:, a + 1, L + a : L + a + 1], in_=ident_f32[:, P - 1 : P])
+        share = keep.tile([P, L, L + 1, L], F32)
+        nc.vector.memset(share[:], 1.0)
+        for a in range(L - 1):
+            nc.vector.memset(share[:, :, a, 0 : L - 1 - a], 0.0)
+        for s in range(L):
+            nc.vector.tensor_scalar_mul(out=share[:, :, :, s], in0=share[:, :, :, s], scalar1=1.0 / (L * (N - s - 1)))
         terms = keep.tile([P, L, L + 1, L + 1], F32)
         nc.vector.memset(terms[:], 0.0)
         nc.vector.memset(terms[:, :, L, L : L + 1], 1.0)
 
-        nc.vector.reciprocal(out=total[:], in_=total[:])
-        iw = keep.tile([P, 2], F32)
-        nc.vector.tensor_scalar_mul(out=iw[:], in0=expd[:], scalar1=total[:, 0:1])
-        bias_pt = keep.tile([P, PACK], F32)
-        nc.vector.tensor_scalar_mul(out=bias_pt[:], in0=b3_pt[:], scalar1=iw[:, 1:2])
-        nc.vector.tensor_scalar_mul(out=kappa[:], in0=kappa[:], scalar1=iw[:, 0:1])
-
         gains = keep.tile([P, B, L, L + 1], F32)
-        sums = {}
-        lacking = {}
+        out_b_all = keep.tile([P, D], F32)
+        w3_codes = keep.tile([P, D], U32, align_bytes=64)
+        w3_scales = keep.tile([P, D], U8, align_bytes=64)
+        ow_codes = keep.tile([P, D], U32, align_bytes=64)
+        ow_scales = keep.tile([P, D], U8, align_bytes=64)
+        iw = keep.tile([P, 2], F32)
+        bias_pt = keep.tile([P, PACK], F32)
+        kappa = keep.tile([P, L, L + 1, L], F32)
 
-        def sum_fields(b):
-            bank = psum_flip.tile([P, L, 2 * L], F32, tag="flipped")
+        weight_banks, weight_grouped = {}, {}
+        sums, lacking = {}, {}
+        field_banks, scaled = {}, {}
+        hidden_banks, h_grouped, h_codes, h_scales = {}, {}, {}, {}
+        nl, fused, e_codes, e_scales, acc = {}, {}, {}, {}, {}
+
+        def flip_weight(key, pool, tag, rows4, half):
+            bank = pool.tile([P, 2, 2, P], F32, tag=tag, name="weight_bank")
+            flip_pair(nc, bank, rows4[:, 2 * half : 2 * half + 2, :], ident_f32)
+            weight_banks[key] = bank
+
+        def copy_weight(key, copy_out):
+            grouped = stage.tile([P, 2, P, PACK], BF16, align_bytes=64, tag="weight_grouped")
+            copy_pair(copy_out, grouped, weight_banks[key])
+            weight_grouped[key] = grouped
+
+        def quantise_weight(key, codes, scales, half):
+            columns = slice(half * PAIR, (half + 1) * PAIR)
+            quantise_pair(nc, weight_grouped[key], codes[:, columns], scales[:, columns])
+
+        def sum_fields(b, pool, tag):
+            bank = pool.tile([P, L, 2 * L], F32, tag=tag, name="sums_bank")
             for t in range(L):
                 for i in range(TILES):
                     nc.tensor.matmul(
@@ -177,118 +173,94 @@ def tile_fieldinteractionoperators_pa_kernel(
             nc.vector.tensor_tensor(out=lack[:], in0=sums[b][:, :, L : 2 * L], in1=gains[:, b, :, 0:L], op=ALU.mult)
             lacking[b] = lack
 
-        field_banks = {}
-        scaled = {}
-        hidden_banks = {}
-        h_grouped = {}
-        h_codes = {}
-        h_scales = {}
+        def flip_fields(r):
+            b, half = divmod(r, 2)
+            bank = psum_flip.tile([P, 2, 2, P], F32, tag="flip", name="field_bank")
+            flip_pair(nc, bank, f_nat[:, b, 2 * half : 2 * half + 2, :], ident_f32)
+            field_banks[r] = bank
+            scaled_r = stage.tile([P, PACK, 2, P], F32, tag="scaled")
+            scaled[r] = scaled_r
 
-        def flip_fields(b):
-            for u in range(2):
-                flipped_f = psum_field.tile([P, TILES, P], F32, tag="fields")
-                for i in range(TILES):
-                    nc.tensor.transpose(flipped_f[:, i, :], alternate_words(f_nat[:, b, i, :], u), ident_f32[:])
-                field_banks[(b, u)] = flipped_f
-            scaled_b = stage.tile([P, PACK, N], F32, tag="scaled")
-            scaled[b] = scaled_b
-
-        def scale_fields(b, t):
+        def scale_fields(r, t):
+            b = r // 2
             u, e = divmod(t, 2)
-            halves = field_banks[(b, u)][:].bitcast(BF16).rearrange("p i (q e) -> p (i q) e", e=2)
+            halves = field_banks[r][:].bitcast(BF16).rearrange("p g u (q e) -> p g u q e", e=2)
             nc.scalar.activation(
-                out=scaled[b][:, t, :],
-                in_=halves[:, :, e],
+                out=scaled[r][:, t],
+                in_=halves[:, :, u, :, e],
                 func=ACT.Identity,
                 scale=gains[:, b, t, L : L + 1] if t < L else 1.0,
                 bias=bias_pt[:, t : t + 1],
             )
 
-        def mend_last_tokens(b):
-            last_columns = scaled[b][:, 0:L, :].rearrange("p t (i q) -> p t i q", q=P)[:, :, 1:TILES, P - 1]
-            nc.vector.tensor_tensor(out=last_columns, in0=last_columns, in1=lacking[b][:], op=ALU.subtract)
+        def mend_last_tokens(r):
+            b, half = divmod(r, 2)
+            tiles, which = (slice(1, 2), slice(0, 1)) if half == 0 else (slice(0, 2), slice(1, L))
+            last = scaled[r][:, 0:L, tiles, P - 1]
+            nc.gpsimd.tensor_tensor(out=last, in0=last, in1=lacking[b][:, :, which], op=ALU.subtract)
 
-        def flip_hidden(b):
-            for pair in range(2):
-                bank = psum_flip.tile([P, 2, 2, P], F32, tag="flipped")
-                flip_two_row_tiles(nc, bank, h_nat[:, b, 2 * pair : 2 * pair + 2, :], alternate_words, ident_f32)
-                hidden_banks[(b, pair)] = bank
-            grouped = stage.tile([P, TILES, P, PACK], BF16, align_bytes=64, tag="grouped")
-            h_grouped[b] = grouped
+        def flip_hidden(r):
+            b, half = divmod(r, 2)
+            bank = psum_flip.tile([P, 2, 2, P], F32, tag="flip", name="hidden_bank")
+            flip_pair(nc, bank, h_nat[:, b, 2 * half : 2 * half + 2, :], ident_f32)
+            hidden_banks[r] = bank
 
-        def copy_hidden(copy_out, b, pair):
-            copy_two_row_tiles(copy_out, h_grouped[b], pair, hidden_banks[(b, pair)])
+        def copy_hidden(r, copy_out):
+            grouped = stage.tile([P, 2, P, PACK], BF16, align_bytes=64, tag="grouped")
+            copy_pair(copy_out, grouped, hidden_banks[r])
+            h_grouped[r] = grouped
 
-        def quantise_hidden(b):
-            codes = stage.tile([P, N], U32, align_bytes=64, tag="h_codes")
-            planes = stage.tile([P, N], U8, align_bytes=64, tag="h_scales")
-            quantise_rows(nc, h_grouped[b], codes[:], planes[:])
-            h_codes[b], h_scales[b] = codes, planes
-
-        def flip_weight(pool, tag, rows4, words):
-            banks = []
-            for pair in range(2):
-                bank = pool.tile([P, 2, 2, P], F32, tag=tag, name="weight_bank")
-                flip_two_row_tiles(nc, bank, rows4[:, 2 * pair : 2 * pair + 2, :], words, ident_f32)
-                banks.append(bank)
-            return banks
-
-        def copy_weight(banks):
-            grouped = stage.tile([P, TILES, P, PACK], BF16, align_bytes=64, tag="grouped")
-            for pair in range(2):
-                copy_two_row_tiles(nc.scalar.copy, grouped, pair, banks[pair])
-            return grouped
-
-        nl = {}
-        enhanced = {}
-        e_codes = {}
-        e_scales = {}
-        acc = {}
+        def quantise_hidden(r):
+            codes = stage.tile([P, PAIR], U32, align_bytes=64, tag="h_codes")
+            planes = stage.tile([P, PAIR], U8, align_bytes=64, tag="h_scales")
+            quantise_pair(nc, h_grouped[r], codes[:], planes[:])
+            h_codes[r], h_scales[r] = codes, planes
 
         def first_product(g):
-            b, i = divmod(g, TILES)
+            r, i = divmod(g, 2)
             tokens = slice(i * P, (i + 1) * P)
-            bank = psum_first.tile([P, PACK, P], F32, tag="nl")
+            bank = psum_first.tile([P, PACK, P], F32, tag="nl", name="nl_bank")
             for t in range(PACK):
                 channels = slice(t * P, (t + 1) * P)
                 nc.tensor.matmul_mx(
                     out=bank[:, t, :],
                     lhsT=w3_codes[:, channels].bitcast(FP8X4),
                     lhsT_scale=w3_scales[:, channels],
-                    rhs=h_codes[b][:, tokens].bitcast(FP8X4),
-                    rhs_scale=h_scales[b][:, tokens],
+                    rhs=h_codes[r][:, tokens].bitcast(FP8X4),
+                    rhs_scale=h_scales[r][:, tokens],
                     start=True,
                     stop=True,
                 )
             nl[g] = bank
 
         def fuse(g):
-            b, i = divmod(g, TILES)
-            fused = results.tile([P, P, PACK], BF16, align_bytes=64, tag="fused")
+            r, i = divmod(g, 2)
+            if i == 0:
+                pair_tile = results.tile([P, 2, P, PACK], BF16, align_bytes=64, tag="fused")
+                fused[r] = pair_tile
             nc.vector.scalar_tensor_tensor(
-                out=fused[:],
+                out=fused[r][:, i],
                 in0=nl[g][:].rearrange("p t q -> p q t"),
                 scalar=iw[:, 1:2],
-                in1=scaled[b][:, :, i * P : (i + 1) * P].rearrange("p t q -> p q t"),
+                in1=scaled[r][:, :, i, :].rearrange("p t q -> p q t"),
                 op0=ALU.mult,
                 op1=ALU.add,
             )
-            enhanced[g] = fused
 
-        def quantise_enhanced(g):
-            codes = results.tile([P, P], U32, align_bytes=64, tag="e_codes")
-            planes = results.tile([P, P], U8, align_bytes=64, tag="e_scales")
-            nc.vector.quantize_mx(
-                out=codes[:].bitcast(FP8X4), scales=planes[:], in_=enhanced[g][:].rearrange("p q t -> p (q t)")
-            )
-            e_codes[g], e_scales[g] = codes, planes
+        def quantise_enhanced(r):
+            codes = results.tile([P, PAIR], U32, align_bytes=64, tag="e_codes")
+            planes = results.tile([P, PAIR], U8, align_bytes=64, tag="e_scales")
+            quantise_pair(nc, fused[r], codes[:], planes[:])
+            e_codes[r], e_scales[r] = codes, planes
 
         def second_product(g):
-            bank = psum_second.tile([P, D], F32, tag="acc")
+            r, i = divmod(g, 2)
+            tokens = slice(i * P, (i + 1) * P)
+            bank = psum_second.tile([P, D], F32, tag="acc", name="acc_bank")
             nc.tensor.matmul_mx(
                 out=bank[:],
-                lhsT=e_codes[g][:].bitcast(FP8X4),
-                lhsT_scale=e_scales[g][:],
+                lhsT=e_codes[r][:, tokens].bitcast(FP8X4),
+                lhsT_scale=e_scales[r][:, tokens],
                 rhs=ow_codes[:].bitcast(FP8X4),
                 rhs_scale=ow_scales[:],
                 start=True,
@@ -299,84 +271,127 @@ def tile_fieldinteractionoperators_pa_kernel(
         def finish(g):
             b, i = divmod(g, TILES)
             result = results.tile([P, D], F32, tag="result")
-            if i in SCALAR_TILES:
-                nc.scalar.copy(out=result[:], in_=acc[g][:])
-                nc.gpsimd.tensor_tensor(out=result[:], in0=result[:], in1=out_b_all[:], op=ALU.add)
-            else:
-                nc.vector.tensor_tensor(out=result[:], in0=acc[g][:], in1=out_b_all[:], op=ALU.add)
+            nc.vector.tensor_tensor(out=result[:], in0=acc[g][:], in1=out_b_all[:], op=ALU.add)
             nc.sync.dma_start(out=out[b].rearrange("(q i) o -> q i o", i=TILES)[:, i, :], in_=result[:])
 
-        sum_fields(0)
+        for half in range(2):
+            flip_weight(("w3", half), psum_first, "nl", w3_nat[:], half)
+        copy_weight(("w3", 0), nc.vector.tensor_copy)
+        copy_weight(("w3", 1), nc.scalar.copy)
+        spread = psum_second.tile([P, ROW_B3 + PACK], F32, tag="acc", name="spread_bank")
+        nc.tensor.matmul(out=spread[:, 0:ROW_B3], lhsT=ones[:], rhs=rows[:, 0:ROW_B3], start=True, stop=True)
+        b3_words = rows[:, ROW_B3 : ROW_B3 + D].rearrange("k (p t) -> k t p", t=PACK)
+        for t in range(PACK):
+            nc.tensor.matmul(
+                out=spread[:, ROW_B3 + t : ROW_B3 + t + 1], lhsT=b3_words[:, t, :], rhs=ones[:, 0:1], start=True, stop=True
+            )
+        flip_fields(0)
+        flip_hidden(0)
+        sum_fields(0, psum_second, "acc")
+        spread_out_b = psum_first.tile([P, D], F32, tag="nl", name="out_b_bank")
+        nc.tensor.matmul(
+            out=spread_out_b[:], lhsT=ones[:], rhs=rows[:, ROW_OUT_B : ROW_OUT_B + D], start=True, stop=True
+        )
+        flip_hidden(1)
+        flip_weight(("ow", 0), psum_second, "acc", ow_nat[:], 0)
+
+        small = keep.tile([P, ROW_B3 + PACK], F32)
+        nc.vector.tensor_copy(out=small[:], in_=spread[:])
+        neg_top = keep.tile([P, 1], F32)
+        mix = small[:, ROW_MIX : ROW_MIX + 2]
+        nc.vector.tensor_scalar(
+            out=neg_top[:], in0=mix[:, 0:1], scalar1=mix[:, 1:2], scalar2=-1.0, op0=ALU.max, op1=ALU.mult
+        )
+        expd = keep.tile([P, 2], F32)
+        total = keep.tile([P, 1], F32)
+        nc.scalar.activation(out=expd[:], in_=mix, func=ACT.Exp, bias=neg_top[:, 0:1], scale=1.0, accum_out=total[:])
+        own_head = ident_f32[:].rearrange("p (h r) -> p h r", r=P // H)[:, :, 0]
+        by_head = keep.tile([P, L * L, H], F32)
+        nc.vector.tensor_tensor(
+            out=by_head[:],
+            in0=small[:, ROW_KERNELS : ROW_KERNELS + H * L * L].rearrange("p (h x) -> p x h", x=L * L),
+            in1=own_head.unsqueeze(1).to_broadcast([P, L * L, H]),
+            op=ALU.mult,
+        )
+        quantise_weight(("w3", 0), w3_codes, w3_scales, 0)
+        kernels_own = keep.tile([P, L, L], F32)
+        nc.vector.tensor_reduce(out=kernels_own[:].rearrange("p l j -> p (l j)"), in_=by_head[:], axis=AXIS.X, op=ALU.add)
+        nc.vector.reciprocal(out=total[:], in_=total[:])
+        quantise_weight(("w3", 1), w3_codes, w3_scales, 1)
+        nc.vector.tensor_scalar_mul(out=iw[:], in0=expd[:], scalar1=total[:, 0:1])
+        nc.vector.tensor_tensor(
+            out=kappa[:],
+            in0=kernels_own[:].rearrange("p s j -> p j s").unsqueeze(2).to_broadcast([P, L, L + 1, L]),
+            in1=share[:],
+            op=ALU.mult,
+        )
+        nc.vector.tensor_scalar_mul(out=bias_pt[:], in0=small[:, ROW_B3 : ROW_B3 + PACK], scalar1=iw[:, 1:2])
+        nc.vector.tensor_scalar_mul(out=kappa[:], in0=kappa[:], scalar1=iw[:, 0:1])
+        copy_hidden(0, nc.scalar.copy)
+        quantise_hidden(0)
         weigh_sums(0)
         add_terms(0)
         find_lacking(0)
-        w3_banks = flip_weight(psum_first, "nl", w3_nat[:], alternate_words)
-        w3_grouped = copy_weight(w3_banks)
-        flip_fields(0)
-        for t in range(PACK):
+        scale_fields(0, L)
+        nc.scalar.copy(out=out_b_all[:], in_=spread_out_b[:])
+        for t in range(L):
             scale_fields(0, t)
-        flip_hidden(0)
-        w3_codes = keep.tile([P, D], U32, align_bytes=64)
-        w3_scales = keep.tile([P, D], U8, align_bytes=64)
-        quantise_rows(nc, w3_grouped, w3_codes[:], w3_scales[:])
-        copy_hidden(nc.vector.tensor_copy, 0, 0)
-        copy_hidden(nc.vector.tensor_copy, 0, 1)
-        ow_banks = flip_weight(psum_second, "acc", ow_nat[:], alternate_words)
-        ow_grouped = copy_weight(ow_banks)
-        sum_fields(1)
-        quantise_hidden(0)
-        weigh_sums(1)
+        mend_last_tokens(0)
         first_product(0)
         first_product(1)
-        add_terms(1)
-        spread_out_b = psum_second.tile([P, D], F32, tag="acc")
-        nc.tensor.matmul(out=spread_out_b[:], lhsT=ones[:], rhs=out_b_row[:], start=True, stop=True)
-        out_b_all = keep.tile([P, D], F32)
-        nc.scalar.copy(out=out_b_all[:], in_=spread_out_b[:])
-        find_lacking(1)
-        flip_hidden(1)
-        fuse(0)
-        first_product(2)
+        copy_weight(("ow", 0), nc.vector.tensor_copy)
         flip_fields(1)
-        ow_codes = keep.tile([P, D], U32, align_bytes=64)
-        ow_scales = keep.tile([P, D], U8, align_bytes=64)
-        quantise_rows(nc, ow_grouped, ow_codes[:], ow_scales[:])
-        mend_last_tokens(0)
-        copy_hidden(nc.scalar.copy, 1, 0)
-        copy_hidden(nc.scalar.copy, 1, 1)
+        flip_weight(("ow", 1), psum_second, "acc", ow_nat[:], 1)
+        copy_hidden(1, nc.scalar.copy)
+        flip_hidden(2)
+        for t in range(PACK):
+            scale_fields(1, t)
+        mend_last_tokens(1)
 
-        for g in range(1, ALL + 2):
-            if batch_due(g, 7) is not None:
-                sum_fields(batch_due(g, 7))
-            if g < ALL:
-                fuse(g)
-            if g < ALL and g % TILES == 0:
-                mend_last_tokens(g // TILES)
-            if batch_due(g, 6) is not None:
-                weigh_sums(batch_due(g, 6))
-            if batch_due(g, 5) is not None:
-                find_lacking(batch_due(g, 5))
-                flip_hidden(batch_due(g, 5))
-            if batch_due(g, 4) is not None:
-                flip_fields(batch_due(g, 4))
-            if g - 1 < ALL:
-                quantise_enhanced(g - 1)
-                second_product(g - 1)
-            if batch_due(g, 6) is not None:
-                add_terms(batch_due(g, 6))
-            if batch_due(g, 3) is not None:
-                quantise_hidden(batch_due(g, 3))
-            if g + 2 < ALL:
-                first_product(g + 2)
-            if g - 2 >= 0:
-                finish(g - 2)
-            if batch_due(g, 4) is not None:
-                copy_hidden(nc.scalar.copy, batch_due(g, 4), 0)
-                copy_hidden(nc.scalar.copy, batch_due(g, 4), 1)
-            if batch_due(g, 3) is not None:
-                scale_fields(batch_due(g, 3), 0)
-                scale_fields(batch_due(g, 3), 1)
-            if batch_due(g, 2) is not None:
-                scale_fields(batch_due(g, 2), 2)
-            if batch_due(g, 1) is not None:
-                scale_fields(batch_due(g, 1), 3)
+        fuse(0)
+        quantise_hidden(1)
+        first_product(2)
+        first_product(3)
+        fuse(1)
+        copy_weight(("ow", 1), nc.vector.tensor_copy)
+        quantise_enhanced(0)
+        sum_fields(1, psum_flip, "flip")
+        flip_fields(2)
+        for half in range(2):
+            quantise_weight(("ow", half), ow_codes, ow_scales, half)
+        copy_hidden(2, nc.scalar.copy)
+
+        for r in range(1, PAIRS + 1):
+            due = (r + 1) // 2 if r % 2 == 1 and r + 1 < PAIRS else None
+            if r < PAIRS:
+                fuse(2 * r)
+            if due is not None:
+                weigh_sums(due)
+            if r + 2 < PAIRS:
+                flip_hidden(r + 2)
+                flip_fields(r + 2)
+            second_product(2 * r - 2)
+            second_product(2 * r - 1)
+            if r + 1 < PAIRS:
+                quantise_hidden(r + 1)
+                first_product(2 * r + 2)
+            if due is not None:
+                add_terms(due)
+            if r < PAIRS:
+                fuse(2 * r + 1)
+            if r + 1 < PAIRS:
+                first_product(2 * r + 3)
+            if due is not None:
+                find_lacking(due)
+            if r % 2 == 0 and r + 2 < PAIRS:
+                sum_fields((r + 2) // 2, psum_flip, "flip")
+            finish(2 * r - 2)
+            if r < PAIRS:
+                quantise_enhanced(r)
+            finish(2 * r - 1)
+            if r + 2 < PAIRS:
+                copy_hidden(r + 2, nc.scalar.copy)
+            if r + 1 < PAIRS:
+                for t in range(PACK):
+                    scale_fields(r + 1, t)
+                mend_last_tokens(r + 1)

@@ -14,6 +14,7 @@ B, N, D, H, L = 4, 512, 512, 8, 3
 P = 128
 PACK = 4
 TILES = 4
+ALL = B * TILES
 PAIR = 2 * P
 PAIRS = B * TILES // 2
 
@@ -52,6 +53,7 @@ def tile_fieldinteractionoperators_pa_kernel(
         tc.tile_pool(name="keep", bufs=1) as keep,
         tc.tile_pool(name="stage", bufs=3) as stage,
         tc.tile_pool(name="results", bufs=4) as results,
+        tc.tile_pool(name="outgoing", bufs=8) as outgoing,
         tc.psum_pool(name="psum_flip", bufs=3) as psum_flip,
         tc.psum_pool(name="psum_first", bufs=3) as psum_first,
         tc.psum_pool(name="psum_second", bufs=2) as psum_second,
@@ -247,11 +249,25 @@ def tile_fieldinteractionoperators_pa_kernel(
                 op1=ALU.add,
             )
 
-        def quantise_enhanced(r):
+        def make_room_for_enhanced(r):
             codes = results.tile([P, PAIR], U32, align_bytes=64, tag="e_codes")
             planes = results.tile([P, PAIR], U8, align_bytes=64, tag="e_scales")
-            quantise_pair(nc, fused[r], codes[:], planes[:])
             e_codes[r], e_scales[r] = codes, planes
+
+        def quantise_enhanced(r):
+            make_room_for_enhanced(r)
+            quantise_pair(nc, fused[r], e_codes[r][:], e_scales[r][:])
+
+        def quantise_enhanced_tile(g):
+            r, i = divmod(g, 2)
+            if i == 0:
+                make_room_for_enhanced(r)
+            tokens = slice(i * P, (i + 1) * P)
+            nc.vector.quantize_mx(
+                out=e_codes[r][:, tokens].bitcast(FP8X4),
+                scales=e_scales[r][:, tokens],
+                in_=fused[r][:, i].rearrange("p q t -> p (q t)"),
+            )
 
         def second_product(g):
             r, i = divmod(g, 2)
@@ -269,9 +285,18 @@ def tile_fieldinteractionoperators_pa_kernel(
             acc[g] = bank
 
         def finish(g):
-            b, i = divmod(g, TILES)
-            result = results.tile([P, D], F32, tag="result")
+            result = outgoing.tile([P, D], F32, tag="result", name="result")
             nc.vector.tensor_tensor(out=result[:], in0=acc[g][:], in1=out_b_all[:], op=ALU.add)
+            store(g, result)
+
+        def finish_without_vector(g):
+            result = outgoing.tile([P, D], F32, tag="result", name="result")
+            nc.scalar.copy(out=result[:], in_=acc[g][:])
+            nc.gpsimd.tensor_tensor(out=result[:], in0=result[:], in1=out_b_all[:], op=ALU.add)
+            store(g, result)
+
+        def store(g, result):
+            b, i = divmod(g, TILES)
             nc.sync.dma_start(out=out[b].rearrange("(q i) o -> q i o", i=TILES)[:, i, :], in_=result[:])
 
         for half in range(2):
@@ -357,41 +382,56 @@ def tile_fieldinteractionoperators_pa_kernel(
         quantise_enhanced(0)
         sum_fields(1, psum_flip, "flip")
         flip_fields(2)
+        flip_hidden(3)
         for half in range(2):
             quantise_weight(("ow", half), ow_codes, ow_scales, half)
         copy_hidden(2, nc.scalar.copy)
+        copy_hidden(3, nc.scalar.copy)
+        quantise_hidden(2)
+        weigh_sums(1)
+        add_terms(1)
+        find_lacking(1)
 
-        for r in range(1, PAIRS + 1):
-            due = (r + 1) // 2 if r % 2 == 1 and r + 1 < PAIRS else None
-            if r < PAIRS:
-                fuse(2 * r)
+        for r in range(1, PAIRS):
+            due = (r + 2) // 2 if r % 2 == 0 and r + 2 < PAIRS else None
+            last = r == PAIRS - 1
+            second_product(2 * r - 1)
+            second_product(2 * r - 2)
+            if not last:
+                first_product(2 * r + 2)
+            fuse(2 * r)
+            if not last:
+                first_product(2 * r + 3)
             if due is not None:
                 weigh_sums(due)
             if r + 2 < PAIRS:
-                flip_hidden(r + 2)
                 flip_fields(r + 2)
-            second_product(2 * r - 2)
-            second_product(2 * r - 1)
-            if r + 1 < PAIRS:
-                quantise_hidden(r + 1)
-                first_product(2 * r + 2)
+            if r + 3 < PAIRS:
+                flip_hidden(r + 3)
+            if r % 2 == 1 and r + 3 < PAIRS:
+                sum_fields((r + 3) // 2, psum_flip, "flip")
+            if last:
+                finish(2 * r - 2)
+                quantise_enhanced_tile(2 * r)
+            fuse(2 * r + 1)
             if due is not None:
                 add_terms(due)
-            if r < PAIRS:
-                fuse(2 * r + 1)
-            if r + 1 < PAIRS:
-                first_product(2 * r + 3)
-            if due is not None:
-                find_lacking(due)
-            if r % 2 == 0 and r + 2 < PAIRS:
-                sum_fields((r + 2) // 2, psum_flip, "flip")
-            finish(2 * r - 2)
-            if r < PAIRS:
-                quantise_enhanced(r)
-            finish(2 * r - 1)
             if r + 2 < PAIRS:
-                copy_hidden(r + 2, nc.scalar.copy)
-            if r + 1 < PAIRS:
+                quantise_hidden(r + 2)
+            if not last:
                 for t in range(PACK):
                     scale_fields(r + 1, t)
                 mend_last_tokens(r + 1)
+            if due is not None:
+                find_lacking(due)
+            finish_without_vector(2 * r - 1)
+            if not last:
+                quantise_enhanced(r)
+                finish(2 * r - 2)
+            else:
+                quantise_enhanced_tile(2 * r + 1)
+            if r + 3 < PAIRS:
+                copy_hidden(r + 3, nc.scalar.copy)
+        for g in (ALL - 2, ALL - 1):
+            second_product(g)
+            finish(g)

@@ -317,8 +317,8 @@ def tile_fieldinteractionoperators_pa_kernel(
         nc.tensor.matmul(
             out=spread_out_b[:], lhsT=ones[:], rhs=rows[:, ROW_OUT_B : ROW_OUT_B + D], start=True, stop=True
         )
-        flip_hidden(1)
         flip_weight(("ow", 0), psum_second, "acc", ow_nat[:], 0)
+        flip_hidden(1)
 
         small = keep.tile([P, ROW_B3 + PACK], F32)
         nc.vector.tensor_copy(out=small[:], in_=spread[:])
@@ -353,85 +353,91 @@ def tile_fieldinteractionoperators_pa_kernel(
         nc.vector.tensor_scalar_mul(out=bias_pt[:], in0=small[:, ROW_B3 : ROW_B3 + PACK], scalar1=iw[:, 1:2])
         nc.vector.tensor_scalar_mul(out=kappa[:], in0=kappa[:], scalar1=iw[:, 0:1])
         copy_hidden(0, nc.scalar.copy)
-        quantise_hidden(0)
         weigh_sums(0)
         add_terms(0)
+        quantise_hidden(0)
         find_lacking(0)
-        scale_fields(0, L)
-        nc.scalar.copy(out=out_b_all[:], in_=spread_out_b[:])
-        for t in range(L):
+        for t in (L, 0, 1, 2):
             scale_fields(0, t)
         mend_last_tokens(0)
         first_product(0)
         first_product(1)
         copy_weight(("ow", 0), nc.vector.tensor_copy)
-        flip_fields(1)
         flip_weight(("ow", 1), psum_second, "acc", ow_nat[:], 1)
+        flip_fields(1)
         copy_hidden(1, nc.scalar.copy)
         flip_hidden(2)
+        nc.scalar.copy(out=out_b_all[:], in_=spread_out_b[:])
+        copy_weight(("ow", 1), nc.scalar.copy)
         for t in range(PACK):
             scale_fields(1, t)
         mend_last_tokens(1)
 
         fuse(0)
+        fuse(1)
+        sum_fields(1, psum_flip, "flip")
         quantise_hidden(1)
         first_product(2)
         first_product(3)
-        fuse(1)
-        copy_weight(("ow", 1), nc.vector.tensor_copy)
         quantise_enhanced(0)
-        sum_fields(1, psum_flip, "flip")
+        weigh_sums(1)
         flip_fields(2)
         flip_hidden(3)
-        for half in range(2):
-            quantise_weight(("ow", half), ow_codes, ow_scales, half)
-        copy_hidden(2, nc.scalar.copy)
-        copy_hidden(3, nc.scalar.copy)
-        quantise_hidden(2)
-        weigh_sums(1)
+        quantise_weight(("ow", 0), ow_codes, ow_scales, 0)
         add_terms(1)
+        quantise_weight(("ow", 1), ow_codes, ow_scales, 1)
         find_lacking(1)
+        copy_hidden(2, nc.scalar.copy)
+        for t in range(PACK):
+            scale_fields(2, t)
+        mend_last_tokens(2)
+        copy_hidden(3, nc.scalar.copy)
 
-        for r in range(1, PAIRS):
+        for r in range(1, PAIRS - 1):
             due = (r + 2) // 2 if r % 2 == 0 and r + 2 < PAIRS else None
-            last = r == PAIRS - 1
+            fuse(2 * r)
+            fuse(2 * r + 1)
+            if r == 1:
+                quantise_hidden(2)
             second_product(2 * r - 1)
             second_product(2 * r - 2)
-            if not last:
-                first_product(2 * r + 2)
-            fuse(2 * r)
-            if not last:
-                first_product(2 * r + 3)
+            first_product(2 * r + 2)
+            first_product(2 * r + 3)
+            if r + 3 < PAIRS:
+                flip_hidden(r + 3)
+            if r + 2 < PAIRS:
+                flip_fields(r + 2)
+            if r % 2 == 1 and r + 3 < PAIRS:
+                sum_fields((r + 3) // 2, psum_flip, "flip")
             if due is not None:
                 weigh_sums(due)
             if r + 2 < PAIRS:
-                flip_fields(r + 2)
-            if r + 3 < PAIRS:
-                flip_hidden(r + 3)
-            if r % 2 == 1 and r + 3 < PAIRS:
-                sum_fields((r + 3) // 2, psum_flip, "flip")
-            if last:
-                finish(2 * r - 2)
-                quantise_enhanced_tile(2 * r)
-            fuse(2 * r + 1)
+                if r > 1:
+                    quantise_hidden(r + 2)
+            quantise_enhanced(r)
             if due is not None:
                 add_terms(due)
-            if r + 2 < PAIRS:
-                quantise_hidden(r + 2)
-            if not last:
+            finish(2 * r - 2)
+            if due is not None:
+                find_lacking(due)
+            if r == 1:
+                quantise_hidden(3)
+            if r > 1:
                 for t in range(PACK):
                     scale_fields(r + 1, t)
                 mend_last_tokens(r + 1)
-            if due is not None:
-                find_lacking(due)
             finish_without_vector(2 * r - 1)
-            if not last:
-                quantise_enhanced(r)
-                finish(2 * r - 2)
-            else:
-                quantise_enhanced_tile(2 * r + 1)
             if r + 3 < PAIRS:
                 copy_hidden(r + 3, nc.scalar.copy)
+
+        second_product(ALL - 3)
+        second_product(ALL - 4)
+        fuse(ALL - 2)
+        finish(ALL - 4)
+        quantise_enhanced_tile(ALL - 2)
+        fuse(ALL - 1)
+        finish_without_vector(ALL - 3)
+        quantise_enhanced_tile(ALL - 1)
         for g in (ALL - 2, ALL - 1):
             second_product(g)
             finish(g)

@@ -18,11 +18,9 @@ ALL = B * TILES
 PAIR = 2 * P
 PAIRS = B * TILES // 2
 
-ROW_KERNELS = 0
-ROW_MIX = 80
-ROW_B3 = 96
-ROW_OUT_B = ROW_B3 + D
-ROW_END = ROW_OUT_B + D
+ROW_MIX = 16
+ROW_AGAIN = 32
+ROW_END = 48
 
 FLOPS = 2 * 2 * B * N * D * D
 
@@ -38,11 +36,11 @@ def flip_pair(nc, bank, rows2, ident_f32):
 
 
 def copy_pair(copy_out, grouped, bank):
-    copy_out(out=grouped[:].bitcast(F32), in_=bank[:].rearrange("p g u r -> p g r u"))
+    copy_out(out=grouped.bitcast(F32), in_=bank[:].rearrange("p g u r -> p g r u"))
 
 
 def quantise_pair(nc, grouped, codes, scales):
-    nc.vector.quantize_mx(out=codes.bitcast(FP8X4), scales=scales, in_=grouped[:].rearrange("p g r t -> p (g r t)"))
+    nc.vector.quantize_mx(out=codes.bitcast(FP8X4), scales=scales, in_=grouped.rearrange("p g r t -> p (g r t)"))
 
 
 def tile_fieldinteractionoperators_pa_kernel(
@@ -60,15 +58,15 @@ def tile_fieldinteractionoperators_pa_kernel(
         tc.manual_schedule(),
     ):
         rows = keep.tile([P, ROW_END], BF16)
-        for first, last in ((0, ROW_B3), (ROW_B3, ROW_END)):
-            nc.vector.memset(rows[:, first:last].bitcast(F32), 0.0)
-        nc.scalar.dma_start(
-            out=rows[0:1, ROW_KERNELS : ROW_KERNELS + H * L * L],
-            in_=corr_kernels.rearrange("h l j -> (h l j)").unsqueeze(0),
-        )
+        nc.vector.memset(rows[:].bitcast(F32), 0.0)
+        nc.scalar.dma_start(out=rows[0:H, 0 : L * L], in_=corr_kernels.rearrange("h l j -> h (l j)"))
         nc.scalar.dma_start(out=rows[0:1, ROW_MIX : ROW_MIX + 2], in_=inter_w.unsqueeze(0))
-        nc.scalar.dma_start(out=rows[0:1, ROW_B3 : ROW_B3 + D], in_=b3.unsqueeze(0))
-        nc.scalar.dma_start(out=rows[0:1, ROW_OUT_B : ROW_OUT_B + D], in_=out_b.unsqueeze(0))
+        nc.scalar.dma_start(out=rows[0:1, ROW_AGAIN : ROW_AGAIN + 1], in_=inter_w[0:1].unsqueeze(0))
+        b3_pt = keep.tile([P, PACK], BF16)
+        nc.scalar.dma_start(out=b3_pt[:], in_=b3.rearrange("(p t) -> p t", t=PACK))
+        out_b_row = keep.tile([P, D], BF16)
+        nc.vector.memset(out_b_row[:].bitcast(F32), 0.0)
+        nc.scalar.dma_start(out=out_b_row[0:1, :], in_=out_b.unsqueeze(0))
 
         f_nat = keep.tile([P, B, TILES, D], BF16)
         h_nat = keep.tile([P, B, TILES, D], BF16)
@@ -95,10 +93,17 @@ def tile_fieldinteractionoperators_pa_kernel(
         make_identity(nc, ident_f32[:])
         ones = keep.tile([P, P], BF16)
         nc.vector.memset(ones[:], 1.0)
+        minus_ones = keep.tile([P, P], BF16)
+        nc.vector.memset(minus_ones[:], -1.0)
+        head_to_partition = keep.tile([P, P], BF16)
+        nc.vector.memset(head_to_partition[:], 0.0)
+        nc.vector.tensor_copy(
+            out=head_to_partition[:].rearrange("k (h r) -> k h r", r=P // H)[:, :, 0], in_=ident_f32[:, 0:H]
+        )
         zero = keep.tile([P, 1], F32)
         nc.vector.memset(zero[:], 0.0)
         warm = keep.tile([P, 1], F32)
-        nc.scalar.activation(out=warm[:], in_=zero[:], func=ACT.Exp)
+        nc.scalar.activation(out=warm[:], in_=zero[:], func=ACT.Sigmoid)
         token_weights = keep.tile([P, TILES, 2 * L], BF16)
         nc.vector.memset(token_weights[:], 0.0)
         nc.vector.memset(token_weights[:, :, 0:L], 1.0)
@@ -115,6 +120,9 @@ def tile_fieldinteractionoperators_pa_kernel(
         terms = keep.tile([P, L, L + 1, L + 1], F32)
         nc.vector.memset(terms[:], 0.0)
         nc.vector.memset(terms[:, :, L, L : L + 1], 1.0)
+        later_terms = keep.tile([P, L, L + 1, L + 1], F32)
+        nc.gpsimd.memset(later_terms[:], 0.0)
+        nc.gpsimd.memset(later_terms[:, :, L, L : L + 1], 1.0)
 
         gains = keep.tile([P, B, L, L + 1], F32)
         out_b_all = keep.tile([P, D], F32)
@@ -129,6 +137,7 @@ def tile_fieldinteractionoperators_pa_kernel(
         weight_banks, weight_grouped = {}, {}
         sums, lacking = {}, {}
         field_banks, scaled = {}, {}
+        rooms = {}
         hidden_banks, h_grouped, h_codes, h_scales = {}, {}, {}, {}
         nl, fused, e_codes, e_scales, acc = {}, {}, {}, {}, {}
 
@@ -139,8 +148,8 @@ def tile_fieldinteractionoperators_pa_kernel(
 
         def copy_weight(key, copy_out):
             grouped = stage.tile([P, 2, P, PACK], BF16, align_bytes=64, tag="weight_grouped")
-            copy_pair(copy_out, grouped, weight_banks[key])
-            weight_grouped[key] = grouped
+            copy_pair(copy_out, grouped[:], weight_banks[key])
+            weight_grouped[key] = grouped[:]
 
         def quantise_weight(key, codes, scales, half):
             columns = slice(half * PAIR, (half + 1) * PAIR)
@@ -169,6 +178,27 @@ def tile_fieldinteractionoperators_pa_kernel(
 
         def add_terms(b):
             nc.vector.tensor_reduce(out=gains[:, b], in_=terms[:], axis=AXIS.X, op=ALU.add)
+
+        def empty_sums(b):
+            copied = stage.tile([P, L, 2 * L], F32, tag="sums_copy", name="sums_copy")
+            nc.scalar.copy(out=copied[:], in_=sums[b][:])
+            sums[b] = copied
+
+        def make_gains_on_gpsimd(b):
+            nc.gpsimd.tensor_tensor(
+                out=later_terms[:, :, :, 0:L],
+                in0=sums[b][:, :, 0:L].unsqueeze(2).to_broadcast([P, L, L + 1, L]),
+                in1=kappa[:],
+                op=ALU.mult,
+            )
+            halves = stage.tile([P, L, L + 1, 2], F32, tag="halves")
+            nc.gpsimd.tensor_tensor(
+                out=halves[:], in0=later_terms[:, :, :, 0:2], in1=later_terms[:, :, :, 2:4], op=ALU.add
+            )
+            nc.gpsimd.tensor_tensor(out=gains[:, b], in0=halves[:, :, :, 0], in1=halves[:, :, :, 1], op=ALU.add)
+            lack = stage.tile([P, L, L], F32, tag="lacking")
+            nc.gpsimd.tensor_tensor(out=lack[:], in0=sums[b][:, :, L : 2 * L], in1=gains[:, b, :, 0:L], op=ALU.mult)
+            lacking[b] = lack
 
         def find_lacking(b):
             lack = stage.tile([P, L, L], F32, tag="lacking")
@@ -207,16 +237,25 @@ def tile_fieldinteractionoperators_pa_kernel(
             flip_pair(nc, bank, h_nat[:, b, 2 * half : 2 * half + 2, :], ident_f32)
             hidden_banks[r] = bank
 
+        def room(r):
+            if r not in rooms:
+                both = results.tile([P, 2, 2, P, PACK], BF16, align_bytes=64, tag="room")
+                rooms[r] = both
+            return rooms[r]
+
         def copy_hidden(r, copy_out):
-            grouped = stage.tile([P, 2, P, PACK], BF16, align_bytes=64, tag="grouped")
-            copy_pair(copy_out, grouped, hidden_banks[r])
-            h_grouped[r] = grouped
+            if r <= 3:
+                grouped = stage.tile([P, 2, P, PACK], BF16, align_bytes=64, tag="grouped")
+                h_grouped[r] = grouped[:]
+            else:
+                h_grouped[r] = room(r - 2)[:, 1]
+            copy_pair(copy_out, h_grouped[r], hidden_banks[r])
 
         def quantise_hidden(r):
             codes = stage.tile([P, PAIR], U32, align_bytes=64, tag="h_codes")
             planes = stage.tile([P, PAIR], U8, align_bytes=64, tag="h_scales")
             quantise_pair(nc, h_grouped[r], codes[:], planes[:])
-            h_codes[r], h_scales[r] = codes, planes
+            h_codes[r], h_scales[r] = codes[:], planes[:]
 
         def first_product(g):
             r, i = divmod(g, 2)
@@ -237,9 +276,7 @@ def tile_fieldinteractionoperators_pa_kernel(
 
         def fuse(g):
             r, i = divmod(g, 2)
-            if i == 0:
-                pair_tile = results.tile([P, 2, P, PACK], BF16, align_bytes=64, tag="fused")
-                fused[r] = pair_tile
+            fused[r] = room(r)[:, 0]
             nc.vector.scalar_tensor_tensor(
                 out=fused[r][:, i],
                 in0=nl[g][:].rearrange("p t q -> p q t"),
@@ -252,22 +289,20 @@ def tile_fieldinteractionoperators_pa_kernel(
         def make_room_for_enhanced(r):
             codes = results.tile([P, PAIR], U32, align_bytes=64, tag="e_codes")
             planes = results.tile([P, PAIR], U8, align_bytes=64, tag="e_scales")
-            e_codes[r], e_scales[r] = codes, planes
+            e_codes[r], e_scales[r] = codes[:], planes[:]
 
         def quantise_enhanced(r):
             make_room_for_enhanced(r)
-            quantise_pair(nc, fused[r], e_codes[r][:], e_scales[r][:])
+            quantise_pair(nc, fused[r], e_codes[r], e_scales[r])
 
-        def quantise_enhanced_tile(g):
-            r, i = divmod(g, 2)
-            if i == 0:
-                make_room_for_enhanced(r)
-            tokens = slice(i * P, (i + 1) * P)
+        def quantise_round(r):
+            codes = results.tile([P, 2 * PAIR], U32, align_bytes=64, tag="codes_of_round")
+            planes = results.tile([P, 2 * PAIR], U8, align_bytes=64, tag="scales_of_round")
             nc.vector.quantize_mx(
-                out=e_codes[r][:, tokens].bitcast(FP8X4),
-                scales=e_scales[r][:, tokens],
-                in_=fused[r][:, i].rearrange("p q t -> p (q t)"),
+                out=codes[:].bitcast(FP8X4), scales=planes[:], in_=rooms[r][:].rearrange("p k g r t -> p (k g r t)")
             )
+            e_codes[r], e_scales[r] = codes[:, 0:PAIR], planes[:, 0:PAIR]
+            h_codes[r + 2], h_scales[r + 2] = codes[:, PAIR : 2 * PAIR], planes[:, PAIR : 2 * PAIR]
 
         def second_product(g):
             r, i = divmod(g, 2)
@@ -284,74 +319,63 @@ def tile_fieldinteractionoperators_pa_kernel(
             )
             acc[g] = bank
 
-        def finish(g):
+        def finish(g, pieces=1):
             result = outgoing.tile([P, D], F32, tag="result", name="result")
-            nc.vector.tensor_tensor(out=result[:], in0=acc[g][:], in1=out_b_all[:], op=ALU.add)
-            store(g, result)
+            width = D // pieces
+            for c in range(0, D, width):
+                columns = slice(c, c + width)
+                nc.vector.tensor_tensor(
+                    out=result[:, columns], in0=acc[g][:, columns], in1=out_b_all[:, columns], op=ALU.add
+                )
+                store(g, result, columns)
 
         def finish_without_vector(g):
             result = outgoing.tile([P, D], F32, tag="result", name="result")
             nc.scalar.copy(out=result[:], in_=acc[g][:])
             nc.gpsimd.tensor_tensor(out=result[:], in0=result[:], in1=out_b_all[:], op=ALU.add)
-            store(g, result)
+            store(g, result, slice(0, D))
 
-        def store(g, result):
+        def store(g, result, columns):
             b, i = divmod(g, TILES)
-            nc.sync.dma_start(out=out[b].rearrange("(q i) o -> q i o", i=TILES)[:, i, :], in_=result[:])
+            nc.sync.dma_start(
+                out=out[b].rearrange("(q i) o -> q i o", i=TILES)[:, i, columns], in_=result[:, columns]
+            )
 
         for half in range(2):
             flip_weight(("w3", half), psum_first, "nl", w3_nat[:], half)
         copy_weight(("w3", 0), nc.vector.tensor_copy)
         copy_weight(("w3", 1), nc.scalar.copy)
-        spread = psum_second.tile([P, ROW_B3 + PACK], F32, tag="acc", name="spread_bank")
-        nc.tensor.matmul(out=spread[:, 0:ROW_B3], lhsT=ones[:], rhs=rows[:, 0:ROW_B3], start=True, stop=True)
-        b3_words = rows[:, ROW_B3 : ROW_B3 + D].rearrange("k (p t) -> k t p", t=PACK)
-        for t in range(PACK):
-            nc.tensor.matmul(
-                out=spread[:, ROW_B3 + t : ROW_B3 + t + 1], lhsT=b3_words[:, t, :], rhs=ones[:, 0:1], start=True, stop=True
-            )
+        spread = psum_second.tile([P, ROW_END], F32, tag="acc", name="spread_bank")
+        kernels_own = spread[:, 0 : L * L]
+        mix = spread[:, ROW_MIX : ROW_MIX + 2]
+        nc.tensor.matmul(out=kernels_own, lhsT=head_to_partition[:], rhs=rows[:, 0 : L * L], start=True, stop=True)
+        nc.tensor.matmul(out=mix, lhsT=ones[:], rhs=rows[:, ROW_MIX : ROW_MIX + 2], start=True, stop=False)
+        nc.tensor.matmul(
+            out=mix,
+            lhsT=minus_ones[:],
+            rhs=rows[:, ROW_MIX + 1 : ROW_AGAIN + 1 : ROW_AGAIN - ROW_MIX - 1],
+            start=False,
+            stop=True,
+        )
         flip_fields(0)
         flip_hidden(0)
         sum_fields(0, psum_second, "acc")
         spread_out_b = psum_first.tile([P, D], F32, tag="nl", name="out_b_bank")
-        nc.tensor.matmul(
-            out=spread_out_b[:], lhsT=ones[:], rhs=rows[:, ROW_OUT_B : ROW_OUT_B + D], start=True, stop=True
-        )
+        nc.tensor.matmul(out=spread_out_b[:], lhsT=ones[:], rhs=out_b_row[:], start=True, stop=True)
         flip_weight(("ow", 0), psum_second, "acc", ow_nat[:], 0)
         flip_hidden(1)
 
-        small = keep.tile([P, ROW_B3 + PACK], F32)
-        nc.vector.tensor_copy(out=small[:], in_=spread[:])
-        neg_top = keep.tile([P, 1], F32)
-        mix = small[:, ROW_MIX : ROW_MIX + 2]
-        nc.vector.tensor_scalar(
-            out=neg_top[:], in0=mix[:, 0:1], scalar1=mix[:, 1:2], scalar2=-1.0, op0=ALU.max, op1=ALU.mult
-        )
-        expd = keep.tile([P, 2], F32)
-        total = keep.tile([P, 1], F32)
-        nc.scalar.activation(out=expd[:], in_=mix, func=ACT.Exp, bias=neg_top[:, 0:1], scale=1.0, accum_out=total[:])
-        own_head = ident_f32[:].rearrange("p (h r) -> p h r", r=P // H)[:, :, 0]
-        by_head = keep.tile([P, L * L, H], F32)
-        nc.vector.tensor_tensor(
-            out=by_head[:],
-            in0=small[:, ROW_KERNELS : ROW_KERNELS + H * L * L].rearrange("p (h x) -> p x h", x=L * L),
-            in1=own_head.unsqueeze(1).to_broadcast([P, L * L, H]),
-            op=ALU.mult,
-        )
-        quantise_weight(("w3", 0), w3_codes, w3_scales, 0)
-        kernels_own = keep.tile([P, L, L], F32)
-        nc.vector.tensor_reduce(out=kernels_own[:].rearrange("p l j -> p (l j)"), in_=by_head[:], axis=AXIS.X, op=ALU.add)
-        nc.vector.reciprocal(out=total[:], in_=total[:])
-        quantise_weight(("w3", 1), w3_codes, w3_scales, 1)
-        nc.vector.tensor_scalar_mul(out=iw[:], in0=expd[:], scalar1=total[:, 0:1])
+        nc.scalar.activation(out=iw[:], in_=mix, func=ACT.Sigmoid)
         nc.vector.tensor_tensor(
             out=kappa[:],
-            in0=kernels_own[:].rearrange("p s j -> p j s").unsqueeze(2).to_broadcast([P, L, L + 1, L]),
+            in0=kernels_own.rearrange("p (s j) -> p j s", j=L).unsqueeze(2).to_broadcast([P, L, L + 1, L]),
             in1=share[:],
             op=ALU.mult,
         )
-        nc.vector.tensor_scalar_mul(out=bias_pt[:], in0=small[:, ROW_B3 : ROW_B3 + PACK], scalar1=iw[:, 1:2])
+        quantise_weight(("w3", 0), w3_codes, w3_scales, 0)
         nc.vector.tensor_scalar_mul(out=kappa[:], in0=kappa[:], scalar1=iw[:, 0:1])
+        nc.vector.tensor_scalar_mul(out=bias_pt[:], in0=b3_pt[:], scalar1=iw[:, 1:2])
+        quantise_weight(("w3", 1), w3_codes, w3_scales, 1)
         copy_hidden(0, nc.scalar.copy)
         weigh_sums(0)
         add_terms(0)
@@ -367,7 +391,6 @@ def tile_fieldinteractionoperators_pa_kernel(
         flip_fields(1)
         copy_hidden(1, nc.scalar.copy)
         flip_hidden(2)
-        nc.scalar.copy(out=out_b_all[:], in_=spread_out_b[:])
         copy_weight(("ow", 1), nc.scalar.copy)
         for t in range(PACK):
             scale_fields(1, t)
@@ -375,23 +398,23 @@ def tile_fieldinteractionoperators_pa_kernel(
 
         fuse(0)
         fuse(1)
-        sum_fields(1, psum_flip, "flip")
         quantise_hidden(1)
         first_product(2)
         first_product(3)
         quantise_enhanced(0)
-        weigh_sums(1)
+        sum_fields(1, psum_flip, "flip")
         flip_fields(2)
         flip_hidden(3)
         quantise_weight(("ow", 0), ow_codes, ow_scales, 0)
-        add_terms(1)
         quantise_weight(("ow", 1), ow_codes, ow_scales, 1)
-        find_lacking(1)
+        nc.vector.tensor_copy(out=out_b_all[:], in_=spread_out_b[:])
         copy_hidden(2, nc.scalar.copy)
+        empty_sums(1)
+        make_gains_on_gpsimd(1)
+        copy_hidden(3, nc.scalar.copy)
         for t in range(PACK):
             scale_fields(2, t)
         mend_last_tokens(2)
-        copy_hidden(3, nc.scalar.copy)
 
         for r in range(1, PAIRS - 1):
             due = (r + 2) // 2 if r % 2 == 0 and r + 2 < PAIRS else None
@@ -409,35 +432,34 @@ def tile_fieldinteractionoperators_pa_kernel(
                 flip_fields(r + 2)
             if r % 2 == 1 and r + 3 < PAIRS:
                 sum_fields((r + 3) // 2, psum_flip, "flip")
-            if due is not None:
-                weigh_sums(due)
-            if r + 2 < PAIRS:
-                if r > 1:
-                    quantise_hidden(r + 2)
-            quantise_enhanced(r)
-            if due is not None:
-                add_terms(due)
+            if r > 1 and r + 2 < PAIRS:
+                quantise_round(r)
+            else:
+                quantise_enhanced(r)
             finish(2 * r - 2)
-            if due is not None:
-                find_lacking(due)
             if r == 1:
                 quantise_hidden(3)
+            if due is not None:
+                empty_sums(due)
             if r > 1:
                 for t in range(PACK):
                     scale_fields(r + 1, t)
                 mend_last_tokens(r + 1)
+            if due is not None:
+                make_gains_on_gpsimd(due)
             finish_without_vector(2 * r - 1)
             if r + 3 < PAIRS:
                 copy_hidden(r + 3, nc.scalar.copy)
 
-        second_product(ALL - 3)
-        second_product(ALL - 4)
-        fuse(ALL - 2)
-        finish(ALL - 4)
-        quantise_enhanced_tile(ALL - 2)
-        fuse(ALL - 1)
-        finish_without_vector(ALL - 3)
-        quantise_enhanced_tile(ALL - 1)
-        for g in (ALL - 2, ALL - 1):
-            second_product(g)
-            finish(g)
+        last = PAIRS - 1
+        second_product(2 * last - 2)
+        second_product(2 * last - 1)
+        fuse(2 * last)
+        fuse(2 * last + 1)
+        quantise_enhanced(last)
+        finish(2 * last - 1)
+        finish_without_vector(2 * last - 2)
+        second_product(2 * last)
+        second_product(2 * last + 1)
+        finish(2 * last)
+        finish(2 * last + 1, pieces=2)

@@ -19,8 +19,7 @@ PAIR = 2 * P
 PAIRS = B * TILES // 2
 
 ROW_MIX = 16
-ROW_AGAIN = 32
-ROW_END = 48
+ROW_END = 32
 
 FLOPS = 2 * 2 * B * N * D * D
 
@@ -59,14 +58,9 @@ def tile_fieldinteractionoperators_pa_kernel(
     ):
         rows = keep.tile([P, ROW_END], BF16)
         nc.vector.memset(rows[:].bitcast(F32), 0.0)
-        nc.scalar.dma_start(out=rows[0:H, 0 : L * L], in_=corr_kernels.rearrange("h l j -> h (l j)"))
-        nc.scalar.dma_start(out=rows[0:1, ROW_MIX : ROW_MIX + 2], in_=inter_w.unsqueeze(0))
-        nc.scalar.dma_start(out=rows[0:1, ROW_AGAIN : ROW_AGAIN + 1], in_=inter_w[0:1].unsqueeze(0))
-        b3_pt = keep.tile([P, PACK], BF16)
-        nc.scalar.dma_start(out=b3_pt[:], in_=b3.rearrange("(p t) -> p t", t=PACK))
         out_b_row = keep.tile([P, D], BF16)
         nc.vector.memset(out_b_row[:].bitcast(F32), 0.0)
-        nc.scalar.dma_start(out=out_b_row[0:1, :], in_=out_b.unsqueeze(0))
+        b3_pt = keep.tile([P, PACK], BF16)
 
         f_nat = keep.tile([P, B, TILES, D], BF16)
         h_nat = keep.tile([P, B, TILES, D], BF16)
@@ -81,10 +75,14 @@ def tile_fieldinteractionoperators_pa_kernel(
         w3_rows = w3.rearrange("(p t) k -> p t k", t=TILES)
         for half in range(2):
             nc.sync.dma_start(out=w3_nat[:, 2 * half : 2 * half + 2], in_=w3_rows[:, 2 * half : 2 * half + 2])
-        load_tokens(f_nat, fields, 0, 0, TILES)
+        nc.sync.dma_start(out=rows[0:H, 0 : L * L], in_=corr_kernels.rearrange("h l j -> h (l j)"))
+        nc.sync.dma_start(out=rows[0:1, ROW_MIX : ROW_MIX + 2], in_=inter_w.unsqueeze(0))
+        nc.sync.dma_start(out=b3_pt[:], in_=b3.rearrange("(p t) -> p t", t=PACK))
         load_tokens(h_nat, h2, 0, 0, 2)
+        load_tokens(f_nat, fields, 0, 0, TILES)
         load_tokens(h_nat, h2, 0, 2, TILES)
         nc.sync.dma_start(out=ow_nat[:], in_=out_w.rearrange("(g r) c -> r g c", r=P))
+        nc.sync.dma_start(out=out_b_row[0:1, :], in_=out_b.unsqueeze(0))
         for b in range(1, B):
             load_tokens(f_nat, fields, b, 0, TILES)
             load_tokens(h_nat, h2, b, 0, TILES)
@@ -341,31 +339,27 @@ def tile_fieldinteractionoperators_pa_kernel(
                 out=out[b].rearrange("(q i) o -> q i o", i=TILES)[:, i, columns], in_=result[:, columns]
             )
 
-        for half in range(2):
-            flip_weight(("w3", half), psum_first, "nl", w3_nat[:], half)
+        flip_weight(("w3", 0), psum_first, "nl", w3_nat[:], 0)
         copy_weight(("w3", 0), nc.vector.tensor_copy)
-        copy_weight(("w3", 1), nc.scalar.copy)
         spread = psum_second.tile([P, ROW_END], F32, tag="acc", name="spread_bank")
         kernels_own = spread[:, 0 : L * L]
-        mix = spread[:, ROW_MIX : ROW_MIX + 2]
+        mix = spread[:, ROW_MIX : ROW_MIX + 1]
         nc.tensor.matmul(out=kernels_own, lhsT=head_to_partition[:], rhs=rows[:, 0 : L * L], start=True, stop=True)
-        nc.tensor.matmul(out=mix, lhsT=ones[:], rhs=rows[:, ROW_MIX : ROW_MIX + 2], start=True, stop=False)
-        nc.tensor.matmul(
-            out=mix,
-            lhsT=minus_ones[:],
-            rhs=rows[:, ROW_MIX + 1 : ROW_AGAIN + 1 : ROW_AGAIN - ROW_MIX - 1],
-            start=False,
-            stop=True,
-        )
-        flip_fields(0)
+        nc.tensor.matmul(out=mix, lhsT=ones[:], rhs=rows[:, ROW_MIX : ROW_MIX + 1], start=True, stop=False)
+        nc.tensor.matmul(out=mix, lhsT=minus_ones[:], rhs=rows[:, ROW_MIX + 1 : ROW_MIX + 2], start=False, stop=True)
+        flip_weight(("w3", 1), psum_first, "nl", w3_nat[:], 1)
+        for c, sign in ((0, 1.0), (1, -1.0)):
+            nc.scalar.activation(out=iw[:, c : c + 1], in_=mix, func=ACT.Sigmoid, scale=sign)
+        copy_weight(("w3", 1), nc.scalar.copy)
         flip_hidden(0)
+        copy_hidden(0, nc.scalar.copy)
         sum_fields(0, psum_second, "acc")
+        flip_fields(0)
+        flip_hidden(1)
+        flip_weight(("ow", 0), psum_second, "acc", ow_nat[:], 0)
         spread_out_b = psum_first.tile([P, D], F32, tag="nl", name="out_b_bank")
         nc.tensor.matmul(out=spread_out_b[:], lhsT=ones[:], rhs=out_b_row[:], start=True, stop=True)
-        flip_weight(("ow", 0), psum_second, "acc", ow_nat[:], 0)
-        flip_hidden(1)
 
-        nc.scalar.activation(out=iw[:], in_=mix, func=ACT.Sigmoid)
         nc.vector.tensor_tensor(
             out=kappa[:],
             in0=kernels_own.rearrange("p (s j) -> p j s", j=L).unsqueeze(2).to_broadcast([P, L, L + 1, L]),
@@ -376,10 +370,9 @@ def tile_fieldinteractionoperators_pa_kernel(
         nc.vector.tensor_scalar_mul(out=kappa[:], in0=kappa[:], scalar1=iw[:, 0:1])
         nc.vector.tensor_scalar_mul(out=bias_pt[:], in0=b3_pt[:], scalar1=iw[:, 1:2])
         quantise_weight(("w3", 1), w3_codes, w3_scales, 1)
-        copy_hidden(0, nc.scalar.copy)
+        quantise_hidden(0)
         weigh_sums(0)
         add_terms(0)
-        quantise_hidden(0)
         find_lacking(0)
         for t in (L, 0, 1, 2):
             scale_fields(0, t)
@@ -391,6 +384,7 @@ def tile_fieldinteractionoperators_pa_kernel(
         flip_fields(1)
         copy_hidden(1, nc.scalar.copy)
         flip_hidden(2)
+        nc.scalar.copy(out=out_b_all[:], in_=spread_out_b[:])
         copy_weight(("ow", 1), nc.scalar.copy)
         for t in range(PACK):
             scale_fields(1, t)
@@ -398,23 +392,23 @@ def tile_fieldinteractionoperators_pa_kernel(
 
         fuse(0)
         fuse(1)
+        sum_fields(1, psum_flip, "flip")
         quantise_hidden(1)
         first_product(2)
         first_product(3)
         quantise_enhanced(0)
-        sum_fields(1, psum_flip, "flip")
+        weigh_sums(1)
         flip_fields(2)
         flip_hidden(3)
         quantise_weight(("ow", 0), ow_codes, ow_scales, 0)
+        add_terms(1)
         quantise_weight(("ow", 1), ow_codes, ow_scales, 1)
-        nc.vector.tensor_copy(out=out_b_all[:], in_=spread_out_b[:])
+        find_lacking(1)
         copy_hidden(2, nc.scalar.copy)
-        empty_sums(1)
-        make_gains_on_gpsimd(1)
-        copy_hidden(3, nc.scalar.copy)
         for t in range(PACK):
             scale_fields(2, t)
         mend_last_tokens(2)
+        copy_hidden(3, nc.scalar.copy)
 
         for r in range(1, PAIRS - 1):
             due = (r + 2) // 2 if r % 2 == 0 and r + 2 < PAIRS else None
@@ -432,21 +426,23 @@ def tile_fieldinteractionoperators_pa_kernel(
                 flip_fields(r + 2)
             if r % 2 == 1 and r + 3 < PAIRS:
                 sum_fields((r + 3) // 2, psum_flip, "flip")
-            if r > 1 and r + 2 < PAIRS:
-                quantise_round(r)
-            else:
-                quantise_enhanced(r)
+            if due is not None:
+                weigh_sums(due)
+            if r + 2 < PAIRS:
+                if r > 1:
+                    quantise_hidden(r + 2)
+            quantise_enhanced(r)
+            if due is not None:
+                add_terms(due)
             finish(2 * r - 2)
+            if due is not None:
+                find_lacking(due)
             if r == 1:
                 quantise_hidden(3)
-            if due is not None:
-                empty_sums(due)
             if r > 1:
                 for t in range(PACK):
                     scale_fields(r + 1, t)
                 mend_last_tokens(r + 1)
-            if due is not None:
-                make_gains_on_gpsimd(due)
             finish_without_vector(2 * r - 1)
             if r + 3 < PAIRS:
                 copy_hidden(r + 3, nc.scalar.copy)

@@ -137,7 +137,7 @@ def tile_fieldinteractionoperators_pa_kernel(
         field_banks, scaled = {}, {}
         rooms = {}
         hidden_banks, h_grouped, h_codes, h_scales = {}, {}, {}, {}
-        nl, fused, e_codes, e_scales, acc = {}, {}, {}, {}, {}
+        nl, fused, e_codes, e_scales, acc, emptied = {}, {}, {}, {}, {}, {}
 
         def flip_weight(key, pool, tag, rows4, half):
             bank = pool.tile([P, 2, 2, P], F32, tag=tag, name="weight_bank")
@@ -327,11 +327,15 @@ def tile_fieldinteractionoperators_pa_kernel(
                 )
                 store(g, result, columns)
 
-        def finish_without_vector(g):
-            result = outgoing.tile([P, D], F32, tag="result", name="result")
-            nc.scalar.copy(out=result[:], in_=acc[g][:])
-            nc.gpsimd.tensor_tensor(out=result[:], in0=result[:], in1=out_b_all[:], op=ALU.add)
-            store(g, result, slice(0, D))
+        def empty_bank(g):
+            emptied_g = outgoing.tile([P, D], F32, tag="emptied")
+            nc.scalar.copy(out=emptied_g[:], in_=acc[g][:])
+            emptied[g] = emptied_g
+
+        def add_out_b(g, r):
+            place = fused[r][:].rearrange("p g q t -> p (g q t)").bitcast(F32)
+            nc.gpsimd.tensor_tensor(out=place, in0=emptied[g][:], in1=out_b_all[:], op=ALU.add)
+            store(g, place, slice(0, D))
 
         def store(g, result, columns):
             b, i = divmod(g, TILES)
@@ -440,10 +444,13 @@ def tile_fieldinteractionoperators_pa_kernel(
             if r == 1:
                 quantise_hidden(3)
             if r > 1:
-                for t in range(PACK):
+                for t in range(L):
                     scale_fields(r + 1, t)
                 mend_last_tokens(r + 1)
-            finish_without_vector(2 * r - 1)
+            empty_bank(2 * r - 1)
+            if r > 1:
+                scale_fields(r + 1, L)
+            add_out_b(2 * r - 1, r)
             if r + 3 < PAIRS:
                 copy_hidden(r + 3, nc.scalar.copy)
 
@@ -454,8 +461,9 @@ def tile_fieldinteractionoperators_pa_kernel(
         fuse(2 * last + 1)
         quantise_enhanced(last)
         finish(2 * last - 1)
-        finish_without_vector(2 * last - 2)
+        empty_bank(2 * last - 2)
         second_product(2 * last)
         second_product(2 * last + 1)
         finish(2 * last)
+        add_out_b(2 * last - 2, last)
         finish(2 * last + 1, pieces=2)

@@ -21,6 +21,8 @@ PAIRS = B * TILES // 2
 ROW_MIX = 16
 ROW_END = 32
 
+WARM_UP = 4
+
 FLOPS = 2 * 2 * B * N * D * D
 
 
@@ -58,6 +60,10 @@ def tile_fieldinteractionoperators_pa_kernel(
     ):
         rows = keep.tile([P, ROW_END], BF16)
         nc.vector.memset(rows[:].bitcast(F32), 0.0)
+        ones = keep.tile([P, P], BF16)
+        nc.vector.memset(ones[:], 1.0)
+        blank = keep.tile([P, D], BF16)
+        nc.vector.memset(blank[:].bitcast(F32), 0.0)
         out_b_row = keep.tile([P, D], BF16)
         nc.vector.memset(out_b_row[:].bitcast(F32), 0.0)
         b3_pt = keep.tile([P, PACK], BF16)
@@ -80,17 +86,15 @@ def tile_fieldinteractionoperators_pa_kernel(
         nc.sync.dma_start(out=b3_pt[:], in_=b3.rearrange("(p t) -> p t", t=PACK))
         load_tokens(h_nat, h2, 0, 0, 2)
         load_tokens(f_nat, fields, 0, 0, TILES)
+        nc.sync.dma_start(out=out_b_row[0:1, :], in_=out_b.unsqueeze(0))
         load_tokens(h_nat, h2, 0, 2, TILES)
         nc.sync.dma_start(out=ow_nat[:], in_=out_w.rearrange("(g r) c -> r g c", r=P))
-        nc.sync.dma_start(out=out_b_row[0:1, :], in_=out_b.unsqueeze(0))
         for b in range(1, B):
             load_tokens(f_nat, fields, b, 0, TILES)
             load_tokens(h_nat, h2, b, 0, TILES)
 
         ident_f32 = keep.tile([P, P], F32)
         make_identity(nc, ident_f32[:])
-        ones = keep.tile([P, P], BF16)
-        nc.vector.memset(ones[:], 1.0)
         minus_ones = keep.tile([P, P], BF16)
         nc.vector.memset(minus_ones[:], -1.0)
         head_to_partition = keep.tile([P, P], BF16)
@@ -293,6 +297,16 @@ def tile_fieldinteractionoperators_pa_kernel(
             make_room_for_enhanced(r)
             quantise_pair(nc, fused[r], e_codes[r], e_scales[r])
 
+        def quantise_enhanced_by_tile(r):
+            make_room_for_enhanced(r)
+            for i in range(2):
+                tokens = slice(i * P, (i + 1) * P)
+                nc.vector.quantize_mx(
+                    out=e_codes[r][:, tokens].bitcast(FP8X4),
+                    scales=e_scales[r][:, tokens],
+                    in_=fused[r][:, i].rearrange("p q t -> p (q t)"),
+                )
+
         def quantise_round(r):
             codes = results.tile([P, 2 * PAIR], U32, align_bytes=64, tag="codes_of_round")
             planes = results.tile([P, 2 * PAIR], U8, align_bytes=64, tag="scales_of_round")
@@ -343,6 +357,9 @@ def tile_fieldinteractionoperators_pa_kernel(
                 out=out[b].rearrange("(q i) o -> q i o", i=TILES)[:, i, columns], in_=result[:, columns]
             )
 
+        warm_bank = psum_flip.tile([P, D], F32, tag="flip", name="warm_bank")
+        for k in range(WARM_UP):
+            nc.tensor.matmul(out=warm_bank[:], lhsT=ones[:], rhs=blank[:], start=True, stop=True)
         flip_weight(("w3", 0), psum_first, "nl", w3_nat[:], 0)
         copy_weight(("w3", 0), nc.vector.tensor_copy)
         spread = psum_second.tile([P, ROW_END], F32, tag="acc", name="spread_bank")
@@ -359,10 +376,10 @@ def tile_fieldinteractionoperators_pa_kernel(
         copy_hidden(0, nc.scalar.copy)
         sum_fields(0, psum_second, "acc")
         flip_fields(0)
-        flip_hidden(1)
-        flip_weight(("ow", 0), psum_second, "acc", ow_nat[:], 0)
         spread_out_b = psum_first.tile([P, D], F32, tag="nl", name="out_b_bank")
         nc.tensor.matmul(out=spread_out_b[:], lhsT=ones[:], rhs=out_b_row[:], start=True, stop=True)
+        flip_hidden(1)
+        flip_weight(("ow", 0), psum_second, "acc", ow_nat[:], 0)
 
         nc.vector.tensor_tensor(
             out=kappa[:],
@@ -374,9 +391,10 @@ def tile_fieldinteractionoperators_pa_kernel(
         nc.vector.tensor_scalar_mul(out=kappa[:], in0=kappa[:], scalar1=iw[:, 0:1])
         nc.vector.tensor_scalar_mul(out=bias_pt[:], in0=b3_pt[:], scalar1=iw[:, 1:2])
         quantise_weight(("w3", 1), w3_codes, w3_scales, 1)
-        quantise_hidden(0)
         weigh_sums(0)
+        quantise_hidden(0)
         add_terms(0)
+        nc.vector.tensor_copy(out=out_b_all[:], in_=spread_out_b[:])
         find_lacking(0)
         for t in (L, 0, 1, 2):
             scale_fields(0, t)
@@ -388,7 +406,6 @@ def tile_fieldinteractionoperators_pa_kernel(
         flip_fields(1)
         copy_hidden(1, nc.scalar.copy)
         flip_hidden(2)
-        nc.scalar.copy(out=out_b_all[:], in_=spread_out_b[:])
         copy_weight(("ow", 1), nc.scalar.copy)
         for t in range(PACK):
             scale_fields(1, t)
@@ -401,17 +418,15 @@ def tile_fieldinteractionoperators_pa_kernel(
         first_product(2)
         first_product(3)
         quantise_enhanced(0)
-        weigh_sums(1)
         flip_fields(2)
         flip_hidden(3)
         quantise_weight(("ow", 0), ow_codes, ow_scales, 0)
-        add_terms(1)
+        weigh_sums(1)
         quantise_weight(("ow", 1), ow_codes, ow_scales, 1)
-        find_lacking(1)
+        add_terms(1)
         copy_hidden(2, nc.scalar.copy)
         for t in range(PACK):
             scale_fields(2, t)
-        mend_last_tokens(2)
         copy_hidden(3, nc.scalar.copy)
 
         for r in range(1, PAIRS - 1):
@@ -435,21 +450,25 @@ def tile_fieldinteractionoperators_pa_kernel(
             if r + 2 < PAIRS:
                 if r > 1:
                     quantise_hidden(r + 2)
+            if r + 2 == PAIRS:
+                finish(2 * r - 2)
             quantise_enhanced(r)
             if due is not None:
                 add_terms(due)
-            finish(2 * r - 2)
+            if r + 2 < PAIRS:
+                finish(2 * r - 2)
             if due is not None:
                 find_lacking(due)
             if r == 1:
+                find_lacking(1)
                 quantise_hidden(3)
             if r > 1:
-                for t in range(L):
+                for t in range(PACK):
                     scale_fields(r + 1, t)
                 mend_last_tokens(r + 1)
+            else:
+                mend_last_tokens(2)
             empty_bank(2 * r - 1)
-            if r > 1:
-                scale_fields(r + 1, L)
             add_out_b(2 * r - 1, r)
             if r + 3 < PAIRS:
                 copy_hidden(r + 3, nc.scalar.copy)
@@ -459,7 +478,7 @@ def tile_fieldinteractionoperators_pa_kernel(
         second_product(2 * last - 1)
         fuse(2 * last)
         fuse(2 * last + 1)
-        quantise_enhanced(last)
+        quantise_enhanced_by_tile(last)
         finish(2 * last - 1)
         empty_bank(2 * last - 2)
         second_product(2 * last)

@@ -378,8 +378,6 @@ def tile_fieldinteractionoperators_pa_kernel(
         flip_fields(0)
         spread_out_b = psum_first.tile([P, D], F32, tag="nl", name="out_b_bank")
         nc.tensor.matmul(out=spread_out_b[:], lhsT=ones[:], rhs=out_b_row[:], start=True, stop=True)
-        flip_hidden(1)
-        flip_weight(("ow", 0), psum_second, "acc", ow_nat[:], 0)
 
         nc.vector.tensor_tensor(
             out=kappa[:],
@@ -401,15 +399,16 @@ def tile_fieldinteractionoperators_pa_kernel(
         mend_last_tokens(0)
         first_product(0)
         first_product(1)
-        copy_weight(("ow", 0), nc.vector.tensor_copy)
-        flip_weight(("ow", 1), psum_second, "acc", ow_nat[:], 1)
+        flip_hidden(1)
+        flip_weight(("ow", 0), psum_second, "acc", ow_nat[:], 0)
         flip_fields(1)
+        flip_weight(("ow", 1), psum_second, "acc", ow_nat[:], 1)
         copy_hidden(1, nc.scalar.copy)
         flip_hidden(2)
-        copy_weight(("ow", 1), nc.scalar.copy)
         for t in range(PACK):
             scale_fields(1, t)
         mend_last_tokens(1)
+        copy_weight(("ow", 1), nc.scalar.copy)
 
         fuse(0)
         fuse(1)
@@ -418,23 +417,27 @@ def tile_fieldinteractionoperators_pa_kernel(
         first_product(2)
         first_product(3)
         quantise_enhanced(0)
+        copy_weight(("ow", 0), nc.vector.tensor_copy)
         flip_fields(2)
         flip_hidden(3)
-        quantise_weight(("ow", 0), ow_codes, ow_scales, 0)
         weigh_sums(1)
-        quantise_weight(("ow", 1), ow_codes, ow_scales, 1)
+        quantise_weight(("ow", 0), ow_codes, ow_scales, 0)
         add_terms(1)
         copy_hidden(2, nc.scalar.copy)
+        fuse(2)
+        quantise_weight(("ow", 1), ow_codes, ow_scales, 1)
+        fuse(3)
         for t in range(PACK):
             scale_fields(2, t)
         copy_hidden(3, nc.scalar.copy)
 
         for r in range(1, PAIRS - 1):
             due = (r + 2) // 2 if r % 2 == 0 and r + 2 < PAIRS else None
-            fuse(2 * r)
-            fuse(2 * r + 1)
             if r == 1:
                 quantise_hidden(2)
+            else:
+                fuse(2 * r)
+                fuse(2 * r + 1)
             second_product(2 * r - 1)
             second_product(2 * r - 2)
             first_product(2 * r + 2)

import concourse.mybir as mybir
from concourse.masks import make_identity

F32 = mybir.dt.float32
BF16 = mybir.dt.bfloat16
U32 = mybir.dt.uint32
U8 = mybir.dt.uint8
FP8X4 = mybir.dt.float8_e4m3fn_x4
ALU = mybir.AluOpType
ACT = mybir.ActivationFunctionType
AXIS = mybir.AxisListType

B, N, D, H, L = 4, 512, 512, 8, 3
P = 128
PACK = 4
TILES = 4
ALL = B * TILES
PAIR = 2 * P
PAIRS = B * TILES // 2

ROW_MIX = 16
ROW_END = 32

WARM_UP = 4

FLOPS = 2 * 2 * B * N * D * D


def alternate_words(rows, u):
    return rows.bitcast(F32).rearrange("r (p u) -> r u p", u=2)[:, u, :]


def flip_pair(nc, bank, rows2, ident_f32):
    for g in range(2):
        for u in range(2):
            nc.tensor.transpose(bank[:, g, u, :], alternate_words(rows2[:, g, :], u), ident_f32[:])


def copy_pair(copy_out, grouped, bank):
    copy_out(out=grouped.bitcast(F32), in_=bank[:].rearrange("p g u r -> p g r u"))


def quantise_pair(nc, grouped, codes, scales):
    nc.vector.quantize_mx(out=codes.bitcast(FP8X4), scales=scales, in_=grouped.rearrange("p g r t -> p (g r t)"))


def tile_fieldinteractionoperators_pa_kernel(
    tc, fields, h2, corr_kernels, w3, b3, out_w, out_b, inter_w, out
):
    nc = tc.nc
    with (
        tc.tile_pool(name="keep", bufs=1) as keep,
        tc.tile_pool(name="stage", bufs=3) as stage,
        tc.tile_pool(name="results", bufs=4) as results,
        tc.tile_pool(name="outgoing", bufs=8) as outgoing,
        tc.psum_pool(name="psum_flip", bufs=3) as psum_flip,
        tc.psum_pool(name="psum_first", bufs=3) as psum_first,
        tc.psum_pool(name="psum_second", bufs=2) as psum_second,
        tc.manual_schedule(),
    ):
        rows = keep.tile([P, ROW_END], BF16)
        nc.vector.memset(rows[:].bitcast(F32), 0.0)
        ones = keep.tile([P, P], BF16)
        nc.vector.memset(ones[:], 1.0)
        blank = keep.tile([P, D], BF16)
        nc.vector.memset(blank[:].bitcast(F32), 0.0)
        out_b_row = keep.tile([P, D], BF16)
        nc.vector.memset(out_b_row[:].bitcast(F32), 0.0)
        b3_pt = keep.tile([P, PACK], BF16)

        f_nat = keep.tile([P, B, TILES, D], BF16)
        h_nat = keep.tile([P, B, TILES, D], BF16)
        w3_nat = keep.tile([P, TILES, D], BF16)
        ow_nat = keep.tile([P, TILES, D], BF16)

        def load_tokens(tile, tensor, b, first, last):
            nc.sync.dma_start(
                out=tile[:, b, first:last], in_=tensor[b].rearrange("(q i) c -> q i c", i=TILES)[:, first:last]
            )

        w3_rows = w3.rearrange("(p t) k -> p t k", t=TILES)
        for half in range(2):
            nc.sync.dma_start(out=w3_nat[:, 2 * half : 2 * half + 2], in_=w3_rows[:, 2 * half : 2 * half + 2])
        nc.sync.dma_start(out=rows[0:H, 0 : L * L], in_=corr_kernels.rearrange("h l j -> h (l j)"))
        nc.sync.dma_start(out=rows[0:1, ROW_MIX : ROW_MIX + 2], in_=inter_w.unsqueeze(0))
        nc.sync.dma_start(out=b3_pt[:], in_=b3.rearrange("(p t) -> p t", t=PACK))
        load_tokens(h_nat, h2, 0, 0, 2)
        load_tokens(f_nat, fields, 0, 0, TILES)
        nc.sync.dma_start(out=out_b_row[0:1, :], in_=out_b.unsqueeze(0))
        load_tokens(h_nat, h2, 0, 2, TILES)
        nc.sync.dma_start(out=ow_nat[:], in_=out_w.rearrange("(g r) c -> r g c", r=P))
        for b in range(1, B):
            load_tokens(f_nat, fields, b, 0, TILES)
            load_tokens(h_nat, h2, b, 0, TILES)

        ident_f32 = keep.tile([P, P], F32)
        make_identity(nc, ident_f32[:])
        minus_ones = keep.tile([P, P], BF16)
        nc.vector.memset(minus_ones[:], -1.0)
        head_to_partition = keep.tile([P, P], BF16)
        nc.vector.memset(head_to_partition[:], 0.0)
        nc.vector.tensor_copy(
            out=head_to_partition[:].rearrange("k (h r) -> k h r", r=P // H)[:, :, 0], in_=ident_f32[:, 0:H]
        )
        zero = keep.tile([P, 1], F32)
        nc.vector.memset(zero[:], 0.0)
        warm = keep.tile([P, 1], F32)
        nc.scalar.activation(out=warm[:], in_=zero[:], func=ACT.Sigmoid)
        token_weights = keep.tile([P, TILES, 2 * L], BF16)
        nc.vector.memset(token_weights[:], 0.0)
        nc.vector.memset(token_weights[:, :, 0:L], 1.0)
        for s in range(L):
            nc.vector.memset(token_weights[0:1, 0 : s + 1, s : s + 1], 0.0)
        for a in range(L):
            nc.vector.tensor_copy(out=token_weights[:, a + 1, L + a : L + a + 1], in_=ident_f32[:, P - 1 : P])
        share = keep.tile([P, L, L + 1, L], F32)
        nc.vector.memset(share[:], 1.0)
        for a in range(L - 1):
            nc.vector.memset(share[:, :, a, 0 : L - 1 - a], 0.0)
        for s in range(L):
            nc.vector.tensor_scalar_mul(out=share[:, :, :, s], in0=share[:, :, :, s], scalar1=1.0 / (L * (N - s - 1)))
        terms = keep.tile([P, L, L + 1, L + 1], F32)
        nc.vector.memset(terms[:], 0.0)
        nc.vector.memset(terms[:, :, L, L : L + 1], 1.0)
        later_terms = keep.tile([P, L, L + 1, L + 1], F32)
        nc.gpsimd.memset(later_terms[:], 0.0)
        nc.gpsimd.memset(later_terms[:, :, L, L : L + 1], 1.0)

        gains = keep.tile([P, B, L, L + 1], F32)
        out_b_all = keep.tile([P, D], F32)
        w3_codes = keep.tile([P, D], U32, align_bytes=64)
        w3_scales = keep.tile([P, D], U8, align_bytes=64)
        ow_codes = keep.tile([P, D], U32, align_bytes=64)
        ow_scales = keep.tile([P, D], U8, align_bytes=64)
        iw = keep.tile([P, 2], F32)
        bias_pt = keep.tile([P, PACK], F32)
        kappa = keep.tile([P, L, L + 1, L], F32)

        weight_banks, weight_grouped = {}, {}
        sums, lacking = {}, {}
        field_banks, scaled = {}, {}
        rooms = {}
        hidden_banks, h_grouped, h_codes, h_scales = {}, {}, {}, {}
        nl, fused, e_codes, e_scales, acc, emptied = {}, {}, {}, {}, {}, {}

        def flip_weight(key, pool, tag, rows4, half):
            bank = pool.tile([P, 2, 2, P], F32, tag=tag, name="weight_bank")
            flip_pair(nc, bank, rows4[:, 2 * half : 2 * half + 2, :], ident_f32)
            weight_banks[key] = bank

        def copy_weight(key, copy_out):
            grouped = stage.tile([P, 2, P, PACK], BF16, align_bytes=64, tag="weight_grouped")
            copy_pair(copy_out, grouped[:], weight_banks[key])
            weight_grouped[key] = grouped[:]

        def quantise_weight(key, codes, scales, half):
            columns = slice(half * PAIR, (half + 1) * PAIR)
            quantise_pair(nc, weight_grouped[key], codes[:, columns], scales[:, columns])

        def sum_fields(b, pool, tag):
            bank = pool.tile([P, L, 2 * L], F32, tag=tag, name="sums_bank")
            for t in range(L):
                for i in range(TILES):
                    nc.tensor.matmul(
                        out=bank[:, t, :],
                        lhsT=f_nat[:, b, i, :].rearrange("q (p t) -> q t p", t=PACK)[:, t, :],
                        rhs=token_weights[:, i, :],
                        start=(i == 0),
                        stop=(i == TILES - 1),
                    )
            sums[b] = bank

        def weigh_sums(b):
            nc.vector.tensor_tensor(
                out=terms[:, :, :, 0:L],
                in0=sums[b][:, :, 0:L].unsqueeze(2).to_broadcast([P, L, L + 1, L]),
                in1=kappa[:],
                op=ALU.mult,
            )

        def add_terms(b):
            nc.vector.tensor_reduce(out=gains[:, b], in_=terms[:], axis=AXIS.X, op=ALU.add)

        def empty_sums(b):
            copied = stage.tile([P, L, 2 * L], F32, tag="sums_copy", name="sums_copy")
            nc.scalar.copy(out=copied[:], in_=sums[b][:])
            sums[b] = copied

        def make_gains_on_gpsimd(b):
            nc.gpsimd.tensor_tensor(
                out=later_terms[:, :, :, 0:L],
                in0=sums[b][:, :, 0:L].unsqueeze(2).to_broadcast([P, L, L + 1, L]),
                in1=kappa[:],
                op=ALU.mult,
            )
            halves = stage.tile([P, L, L + 1, 2], F32, tag="halves")
            nc.gpsimd.tensor_tensor(
                out=halves[:], in0=later_terms[:, :, :, 0:2], in1=later_terms[:, :, :, 2:4], op=ALU.add
            )
            nc.gpsimd.tensor_tensor(out=gains[:, b], in0=halves[:, :, :, 0], in1=halves[:, :, :, 1], op=ALU.add)
            lack = stage.tile([P, L, L], F32, tag="lacking")
            nc.gpsimd.tensor_tensor(out=lack[:], in0=sums[b][:, :, L : 2 * L], in1=gains[:, b, :, 0:L], op=ALU.mult)
            lacking[b] = lack

        def find_lacking(b):
            lack = stage.tile([P, L, L], F32, tag="lacking")
            nc.vector.tensor_tensor(out=lack[:], in0=sums[b][:, :, L : 2 * L], in1=gains[:, b, :, 0:L], op=ALU.mult)
            lacking[b] = lack

        def flip_fields(r):
            b, half = divmod(r, 2)
            bank = psum_flip.tile([P, 2, 2, P], F32, tag="flip", name="field_bank")
            flip_pair(nc, bank, f_nat[:, b, 2 * half : 2 * half + 2, :], ident_f32)
            field_banks[r] = bank
            scaled_r = stage.tile([P, PACK, 2, P], F32, tag="scaled")
            scaled[r] = scaled_r

        def scale_fields(r, t):
            b = r // 2
            u, e = divmod(t, 2)
            halves = field_banks[r][:].bitcast(BF16).rearrange("p g u (q e) -> p g u q e", e=2)
            nc.scalar.activation(
                out=scaled[r][:, t],
                in_=halves[:, :, u, :, e],
                func=ACT.Identity,
                scale=gains[:, b, t, L : L + 1] if t < L else 1.0,
                bias=bias_pt[:, t : t + 1],
            )

        def mend_last_tokens(r):
            b, half = divmod(r, 2)
            tiles, which = (slice(1, 2), slice(0, 1)) if half == 0 else (slice(0, 2), slice(1, L))
            last = scaled[r][:, 0:L, tiles, P - 1]
            nc.gpsimd.tensor_tensor(out=last, in0=last, in1=lacking[b][:, :, which], op=ALU.subtract)

        def flip_hidden(r):
            b, half = divmod(r, 2)
            bank = psum_flip.tile([P, 2, 2, P], F32, tag="flip", name="hidden_bank")
            flip_pair(nc, bank, h_nat[:, b, 2 * half : 2 * half + 2, :], ident_f32)
            hidden_banks[r] = bank

        def room(r):
            if r not in rooms:
                both = results.tile([P, 2, 2, P, PACK], BF16, align_bytes=64, tag="room")
                rooms[r] = both
            return rooms[r]

        def copy_hidden(r, copy_out):
            if r <= 3:
                grouped = stage.tile([P, 2, P, PACK], BF16, align_bytes=64, tag="grouped")
                h_grouped[r] = grouped[:]
            else:
                h_grouped[r] = room(r - 2)[:, 1]
            copy_pair(copy_out, h_grouped[r], hidden_banks[r])

        def quantise_hidden(r):
            codes = stage.tile([P, PAIR], U32, align_bytes=64, tag="h_codes")
            planes = stage.tile([P, PAIR], U8, align_bytes=64, tag="h_scales")
            quantise_pair(nc, h_grouped[r], codes[:], planes[:])
            h_codes[r], h_scales[r] = codes[:], planes[:]

        def first_product(g):
            r, i = divmod(g, 2)
            tokens = slice(i * P, (i + 1) * P)
            bank = psum_first.tile([P, PACK, P], F32, tag="nl", name="nl_bank")
            for t in range(PACK):
                channels = slice(t * P, (t + 1) * P)
                nc.tensor.matmul_mx(
                    out=bank[:, t, :],
                    lhsT=w3_codes[:, channels].bitcast(FP8X4),
                    lhsT_scale=w3_scales[:, channels],
                    rhs=h_codes[r][:, tokens].bitcast(FP8X4),
                    rhs_scale=h_scales[r][:, tokens],
                    start=True,
                    stop=True,
                )
            nl[g] = bank

        def fuse(g):
            r, i = divmod(g, 2)
            fused[r] = room(r)[:, 0]
            nc.vector.scalar_tensor_tensor(
                out=fused[r][:, i],
                in0=nl[g][:].rearrange("p t q -> p q t"),
                scalar=iw[:, 1:2],
                in1=scaled[r][:, :, i, :].rearrange("p t q -> p q t"),
                op0=ALU.mult,
                op1=ALU.add,
            )

        def make_room_for_enhanced(r):
            codes = results.tile([P, PAIR], U32, align_bytes=64, tag="e_codes")
            planes = results.tile([P, PAIR], U8, align_bytes=64, tag="e_scales")
            e_codes[r], e_scales[r] = codes[:], planes[:]

        def quantise_enhanced(r):
            make_room_for_enhanced(r)
            quantise_pair(nc, fused[r], e_codes[r], e_scales[r])

        def quantise_enhanced_by_tile(r):
            make_room_for_enhanced(r)
            for i in range(2):
                tokens = slice(i * P, (i + 1) * P)
                nc.vector.quantize_mx(
                    out=e_codes[r][:, tokens].bitcast(FP8X4),
                    scales=e_scales[r][:, tokens],
                    in_=fused[r][:, i].rearrange("p q t -> p (q t)"),
                )

        def quantise_round(r):
            codes = results.tile([P, 2 * PAIR], U32, align_bytes=64, tag="codes_of_round")
            planes = results.tile([P, 2 * PAIR], U8, align_bytes=64, tag="scales_of_round")
            nc.vector.quantize_mx(
                out=codes[:].bitcast(FP8X4), scales=planes[:], in_=rooms[r][:].rearrange("p k g r t -> p (k g r t)")
            )
            e_codes[r], e_scales[r] = codes[:, 0:PAIR], planes[:, 0:PAIR]
            h_codes[r + 2], h_scales[r + 2] = codes[:, PAIR : 2 * PAIR], planes[:, PAIR : 2 * PAIR]

        def second_product(g):
            r, i = divmod(g, 2)
            tokens = slice(i * P, (i + 1) * P)
            bank = psum_second.tile([P, D], F32, tag="acc", name="acc_bank")
            nc.tensor.matmul_mx(
                out=bank[:],
                lhsT=e_codes[r][:, tokens].bitcast(FP8X4),
                lhsT_scale=e_scales[r][:, tokens],
                rhs=ow_codes[:].bitcast(FP8X4),
                rhs_scale=ow_scales[:],
                start=True,
                stop=True,
            )
            acc[g] = bank

        def finish(g, pieces=1):
            result = outgoing.tile([P, D], F32, tag="result", name="result")
            width = D // pieces
            for c in range(0, D, width):
                columns = slice(c, c + width)
                nc.vector.tensor_tensor(
                    out=result[:, columns], in0=acc[g][:, columns], in1=out_b_all[:, columns], op=ALU.add
                )
                store(g, result, columns)

        def empty_bank(g):
            emptied_g = outgoing.tile([P, D], F32, tag="emptied")
            nc.scalar.copy(out=emptied_g[:], in_=acc[g][:])
            emptied[g] = emptied_g

        def add_out_b(g, r):
            place = fused[r][:].rearrange("p g q t -> p (g q t)").bitcast(F32)
            nc.gpsimd.tensor_tensor(out=place, in0=emptied[g][:], in1=out_b_all[:], op=ALU.add)
            store(g, place, slice(0, D))

        def store(g, result, columns):
            b, i = divmod(g, TILES)
            nc.sync.dma_start(
                out=out[b].rearrange("(q i) o -> q i o", i=TILES)[:, i, columns], in_=result[:, columns]
            )

        warm_bank = psum_flip.tile([P, D], F32, tag="flip", name="warm_bank")
        for k in range(WARM_UP):
            nc.tensor.matmul(out=warm_bank[:], lhsT=ones[:], rhs=blank[:], start=True, stop=True)
        flip_weight(("w3", 0), psum_first, "nl", w3_nat[:], 0)
        copy_weight(("w3", 0), nc.vector.tensor_copy)
        spread = psum_second.tile([P, ROW_END], F32, tag="acc", name="spread_bank")
        kernels_own = spread[:, 0 : L * L]
        mix = spread[:, ROW_MIX : ROW_MIX + 1]
        nc.tensor.matmul(out=kernels_own, lhsT=head_to_partition[:], rhs=rows[:, 0 : L * L], start=True, stop=True)
        nc.tensor.matmul(out=mix, lhsT=ones[:], rhs=rows[:, ROW_MIX : ROW_MIX + 1], start=True, stop=False)
        nc.tensor.matmul(out=mix, lhsT=minus_ones[:], rhs=rows[:, ROW_MIX + 1 : ROW_MIX + 2], start=False, stop=True)
        flip_weight(("w3", 1), psum_first, "nl", w3_nat[:], 1)
        for c, sign in ((0, 1.0), (1, -1.0)):
            nc.scalar.activation(out=iw[:, c : c + 1], in_=mix, func=ACT.Sigmoid, scale=sign)
        copy_weight(("w3", 1), nc.scalar.copy)
        flip_hidden(0)
        copy_hidden(0, nc.scalar.copy)
        sum_fields(0, psum_second, "acc")
        flip_fields(0)
        spread_out_b = psum_first.tile([P, D], F32, tag="nl", name="out_b_bank")
        nc.tensor.matmul(out=spread_out_b[:], lhsT=ones[:], rhs=out_b_row[:], start=True, stop=True)

        nc.vector.tensor_tensor(
            out=kappa[:],
            in0=kernels_own.rearrange("p (s j) -> p j s", j=L).unsqueeze(2).to_broadcast([P, L, L + 1, L]),
            in1=share[:],
            op=ALU.mult,
        )
        quantise_weight(("w3", 0), w3_codes, w3_scales, 0)
        nc.vector.tensor_scalar_mul(out=kappa[:], in0=kappa[:], scalar1=iw[:, 0:1])
        nc.vector.tensor_scalar_mul(out=bias_pt[:], in0=b3_pt[:], scalar1=iw[:, 1:2])
        quantise_weight(("w3", 1), w3_codes, w3_scales, 1)
        weigh_sums(0)
        quantise_hidden(0)
        add_terms(0)
        nc.vector.tensor_copy(out=out_b_all[:], in_=spread_out_b[:])
        find_lacking(0)
        for t in (L, 0, 1, 2):
            scale_fields(0, t)
        mend_last_tokens(0)
        first_product(0)
        first_product(1)
        flip_hidden(1)
        flip_weight(("ow", 0), psum_second, "acc", ow_nat[:], 0)
        flip_fields(1)
        flip_weight(("ow", 1), psum_second, "acc", ow_nat[:], 1)
        copy_hidden(1, nc.scalar.copy)
        flip_hidden(2)
        for t in range(PACK):
            scale_fields(1, t)
        mend_last_tokens(1)
        copy_weight(("ow", 1), nc.scalar.copy)

        fuse(0)
        fuse(1)
        sum_fields(1, psum_flip, "flip")
        quantise_hidden(1)
        first_product(2)
        first_product(3)
        quantise_enhanced(0)
        copy_weight(("ow", 0), nc.vector.tensor_copy)
        flip_fields(2)
        flip_hidden(3)
        weigh_sums(1)
        quantise_weight(("ow", 0), ow_codes, ow_scales, 0)
        add_terms(1)
        copy_hidden(2, nc.scalar.copy)
        fuse(2)
        quantise_weight(("ow", 1), ow_codes, ow_scales, 1)
        fuse(3)
        for t in range(PACK):
            scale_fields(2, t)
        copy_hidden(3, nc.scalar.copy)

        for r in range(1, PAIRS - 1):
            due = (r + 2) // 2 if r % 2 == 0 and r + 2 < PAIRS else None
            if r == 1:
                quantise_hidden(2)
            else:
                fuse(2 * r)
                fuse(2 * r + 1)
            second_product(2 * r - 1)
            second_product(2 * r - 2)
            first_product(2 * r + 2)
            first_product(2 * r + 3)
            if r + 3 < PAIRS:
                flip_hidden(r + 3)
            if r + 2 < PAIRS:
                flip_fields(r + 2)
            if r % 2 == 1 and r + 3 < PAIRS:
                sum_fields((r + 3) // 2, psum_flip, "flip")
            if due is not None:
                weigh_sums(due)
            if r + 2 < PAIRS:
                if r > 1:
                    quantise_hidden(r + 2)
            if r + 2 == PAIRS:
                finish(2 * r - 2)
            quantise_enhanced(r)
            if due is not None:
                add_terms(due)
            if r + 2 < PAIRS:
                finish(2 * r - 2)
            if due is not None:
                find_lacking(due)
            if r == 1:
                find_lacking(1)
                quantise_hidden(3)
            if r > 1:
                for t in range(PACK):
                    scale_fields(r + 1, t)
                mend_last_tokens(r + 1)
            else:
                mend_last_tokens(2)
            empty_bank(2 * r - 1)
            add_out_b(2 * r - 1, r)
            if r + 3 < PAIRS:
                copy_hidden(r + 3, nc.scalar.copy)

        last = PAIRS - 1
        second_product(2 * last - 2)
        second_product(2 * last - 1)
        fuse(2 * last)
        fuse(2 * last + 1)
        quantise_enhanced_by_tile(last)
        finish(2 * last - 1)
        empty_bank(2 * last - 2)
        second_product(2 * last)
        second_product(2 * last + 1)
        finish(2 * last)
        add_out_b(2 * last - 2, last)
        finish(2 * last + 1, pieces=2)
